import numpy as np
import ml_dtypes


def mxq(x, axis, fmt="e4m3"):
    dtype, down = {"e4m3": (ml_dtypes.float8_e4m3fn, 7), "e5m2": (ml_dtypes.float8_e5m2, 14)}[fmt]
    v = np.moveaxis(np.asarray(x, np.float32).astype(ml_dtypes.bfloat16).astype(np.float64), axis, -1)
    blocks = v.reshape(v.shape[:-1] + (-1, 32))
    amax = np.abs(blocks).max(-1, keepdims=True)
    byte = np.maximum(np.where(amax > 0, np.frexp(amax)[1] - 1 + 127, 0) - down, 1)
    scale = np.exp2(byte - 127.0)
    codes = (blocks / scale).astype(np.float32).astype(dtype).astype(np.float64)
    return np.moveaxis((codes * scale).reshape(v.shape), -1, axis)


WIDE = False


def mx_kscale(k):
    if not WIDE:
        return np.ones(k)
    levels = np.array([10, -10, 5, -5, 0])
    a = np.random.permutation(np.resize(levels, k // 512 * 4)).reshape(k // 512, 4)
    idx = np.arange(k)
    return np.exp2(a[idx // 512, idx % 128 // 32])


BF16 = ml_dtypes.bfloat16


def bf(x):
    return np.asarray(x, np.float32).astype(BF16)


def f64(x):
    return np.asarray(x).astype(np.float64)


B, Q, K, D = 2, 512, 1024, 1024
NEG = -10000.0


def setup_inputs():
    s, t = mx_kscale(D), mx_kscale(D)
    return {"query": bf(np.random.standard_normal((B, Q, D)) * s),
            "context": bf(np.random.standard_normal((B, K, D)) * 0.5 / t),
            "query_bit": bf(np.random.random((B, Q)) > 0.25),
            "context_bit": bf(np.random.random((B, K)) > 0.25),
            "W_in": bf(np.random.standard_normal((D, D)) * 4.0 / D * t[:, None] / s[None, :]),
            "b_in": bf(np.random.standard_normal(D) / np.sqrt(D) * t)}


def reference(query, context, query_bit, context_bit, W_in, b_in):
    ext = (1.0 - f64(query_bit)[:, :, None] * f64(context_bit)[:, None, :]) * NEG
    q = (mxq(f64(query), 2, "e4m3") @ mxq(f64(W_in), 1, "e4m3").T) + f64(b_in)
    scores = (mxq(q, 2, "e4m3") @ mxq(f64(context), 2, "e4m3").transpose(0, 2, 1)) + ext
    e = np.exp(scores - scores.max(-1, keepdims=True))
    return e / e.sum(-1, keepdims=True)

@@ -1,0 +1,228 @@
+from contextlib import ExitStack
+
+import concourse.mybir as mybir
+from concourse.masks import make_identity
+
+F32 = mybir.dt.float32
+BF16 = mybir.dt.bfloat16
+U32 = mybir.dt.uint32
+U8 = mybir.dt.uint8
+FP8X4 = mybir.dt.float8_e4m3fn_x4
+ALU = mybir.AluOpType
+ACT = mybir.ActivationFunctionType
+AX = mybir.AxisListType
+
+P = 128
+FLOPS = 2 * 1024 * 1024 * 1024 + 2 * 2 * 512 * 1024 * 1024
+
+PIN = False
+ROUTE = {(0, 0): "S", (0, 1): "S", (1, 0): "S", (1, 1): "S"}
+NORM = {0: "G", 1: "G"}
+LOAD_ORDER = ["q0", "W0", "W1", "c00", "c01", "q1", "c10", "c11"]
+
+
+def tile_attention_pa_kernel(tc, query, context, query_bit, context_bit, W_in, b_in, out):
+    nc = tc.nc
+    with ExitStack() as ctx:
+        const = ctx.enter_context(tc.tile_pool(name="const", bufs=1))
+        raw = ctx.enter_context(tc.tile_pool(name="raw", bufs=1))
+        keep = ctx.enter_context(tc.tile_pool(name="keep", bufs=1))
+        stage = ctx.enter_context(tc.tile_pool(name="stage", bufs=4))
+        soft = ctx.enter_context(tc.tile_pool(name="soft", bufs=8))
+        small = ctx.enter_context(tc.tile_pool(name="small", bufs=8))
+        ps_tp = ctx.enter_context(tc.psum_pool(name="ps_tp", bufs=4))
+        ps_mm = ctx.enter_context(tc.psum_pool(name="ps_mm", bufs=4))
+        if PIN:
+            ctx.enter_context(tc.manual_schedule())
+
+        bits = const.tile([P, 2048], BF16, name="bits")
+        nc.vector.memset(bits[:], 0.0)
+        ones = const.tile([P, P], BF16, name="ones")
+        nc.vector.memset(ones[:], 1.0)
+        qb_raw = const.tile([P, 8], BF16, name="qb_raw")
+        b_raw = const.tile([P, 8], BF16, name="b_raw")
+
+        def small_loads():
+            nc.sync.dma_start(
+                out=b_raw[:].rearrange("p (k e) -> p k e", k=4),
+                in_=b_in.rearrange("(k p e) -> p k e", k=4, e=2),
+            )
+            nc.sync.dma_start(out=bits[0:1, :], in_=context_bit.rearrange("(o b) j -> o (b j)", o=1))
+            nc.sync.dma_start(
+                out=qb_raw[:].rearrange("p (b n) -> p b n", b=2),
+                in_=query_bit.rearrange("b (p n) -> p b n", n=4),
+            )
+
+        ident = const.tile([P, P], F32, name="ident")
+        make_identity(nc, ident[:])
+
+        rawt = {}
+        for x in LOAD_ORDER:
+            rawt[x] = raw.tile([P, 4096], BF16, name="raw_" + x)
+            for a2 in range(2):
+                if x[0] == "q":
+                    src = query[int(x[1])].rearrange("(p n) d -> p n d", n=4)[:, 2 * a2 : 2 * a2 + 2, :]
+                elif x[0] == "W":
+                    blk = 2 * int(x[1]) + a2
+                    src = W_in[256 * blk : 256 * blk + 256, :].rearrange("(p e) d -> p e d", e=2)
+                else:
+                    r0 = 512 * int(x[2]) + 256 * a2
+                    src = context[int(x[1]), r0 : r0 + 256, :].rearrange("(c p) e -> p c e", p=P)
+                nc.sync.dma_start(
+                    out=rawt[x][:, 2048 * a2 : 2048 * a2 + 2048].rearrange("p (n d) -> p n d", n=2), in_=src
+                )
+            if x == "W0":
+                small_loads()
+
+        s10k = const.tile([P, 8], F32, name="s10k")
+        nc.vector.tensor_scalar(out=s10k[:], in0=qb_raw[:], scalar1=10000.0, scalar2=None, op0=ALU.mult)
+        bias_f = const.tile([P, 8], F32, name="bias_f")
+        nc.vector.tensor_copy(out=bias_f[:], in_=b_raw[:])
+
+        cbm = const.tile([P, 2048], BF16, name="cbm")
+
+        def spread_mask():
+          for c4 in range(4):
+            pb = ps_mm.tile([P, 512], F32, name="pb", tag="mm")
+            nc.tensor.matmul(out=pb[:], lhsT=ones[:], rhs=bits[:, 512 * c4 : 512 * c4 + 512], start=True, stop=True)
+            if c4 % 2 == 0:
+                nc.vector.tensor_scalar(
+                    out=cbm[:, 512 * c4 : 512 * c4 + 512], in0=pb[:], scalar1=-1.0, scalar2=None, op0=ALU.add
+                )
+            else:
+                nc.scalar.activation(out=cbm[:, 512 * c4 : 512 * c4 + 512], in_=pb[:], func=ACT.Copy, bias=-1.0, scale=1.0)
+
+        codes = {}
+        scales = {}
+
+        def new_codes(key):
+            codes[key] = keep.tile([P, 512], U32, name="c_%s_%d" % key, align_bytes=64)
+            scales[key] = keep.tile([P, 512], U8, name="s_%s_%d" % key, align_bytes=64)
+
+        def quantise(key, grouped):
+            new_codes(key)
+            nc.vector.quantize_mx(out=codes[key][:].bitcast(FP8X4), scales=scales[key][:], in_=grouped[:])
+
+        def mx(acc, wkey, wcols, mkey, mcols, start, stop):
+            nc.tensor.matmul_mx(
+                out=acc,
+                lhsT=codes[wkey][:, wcols].bitcast(FP8X4),
+                lhsT_scale=scales[wkey][:, wcols],
+                rhs=codes[mkey][:, mcols].bitcast(FP8X4),
+                rhs_scale=scales[mkey][:, mcols],
+                start=start,
+                stop=stop,
+            )
+
+        def prep(x, early):
+            words = rawt[x][:].bitcast(F32)
+            for g in range(2):
+                grouped = stage.tile([P, 2048], BF16, name="grp", tag="grp", align_bytes=64)
+                for a2 in range(2):
+                    tp = ps_tp.tile([P, 512], F32, name="tp", tag="tp")
+                    for a in range(2):
+                        for u in range(2):
+                            col = (2 * a2 + a) * 512 + g * 256 + u * 128
+                            nc.tensor.transpose(
+                                tp[:, (2 * a + u) * 128 : (2 * a + u) * 128 + 128], words[:, col : col + 128], ident[:]
+                            )
+                    dst = grouped[:].bitcast(F32)[:, 512 * a2 : 512 * a2 + 512].rearrange(
+                        "p (a r u) -> p a r u", a=2, u=2
+                    )
+                    srcv = tp[:].rearrange("p (a u r) -> p a r u", a=2, u=2)
+                    if early and a2 == 1:
+                        nc.vector.tensor_copy(out=dst, in_=srcv)
+                    else:
+                        nc.scalar.copy(out=dst, in_=srcv)
+                quantise((x, g), grouped)
+
+        def stage1(b, g2):
+            qg = stage.tile([P, 2048], BF16, name="qg", tag="qg", bufs=2, align_bytes=64)
+            wx = "W%d" % g2
+            qx = "q%d" % b
+            if ROUTE[(b, g2)] == "V":
+                for n in range(4):
+                    acc = ps_mm.tile([P, 512], F32, name="acc1", tag="mm")
+                    for t in range(4):
+                        for g in range(2):
+                            mx(
+                                acc[:, 128 * t : 128 * t + 128],
+                                (wx, g), slice(128 * t, 128 * t + 128),
+                                (qx, g), slice(128 * n, 128 * n + 128),
+                                g == 0, g == 1,
+                            )
+                    nc.vector.tensor_tensor(
+                        out=qg[:, 512 * n : 512 * n + 512].rearrange("p (i t) -> p i t", t=4),
+                        in0=acc[:].rearrange("p (t i) -> p i t", t=4),
+                        in1=bias_f[:, 4 * g2 : 4 * g2 + 4].unsqueeze(1).to_broadcast([P, 128, 4]),
+                        op=ALU.add,
+                    )
+            else:
+                qp = stage.tile([P, 2048], BF16, name="qp", tag="qp", bufs=2)
+                for t in range(4):
+                    acc = ps_mm.tile([P, 512], F32, name="acc1", tag="mm")
+                    for g in range(2):
+                        mx(acc[:], (wx, g), slice(128 * t, 128 * t + 128), (qx, g), slice(0, 512), g == 0, g == 1)
+                    nc.scalar.activation(
+                        out=qp[:, 512 * t : 512 * t + 512], in_=acc[:], func=ACT.Identity,
+                        bias=bias_f[:, 4 * g2 + t : 4 * g2 + t + 1], scale=1.0,
+                    )
+                nc.vector.tensor_copy(
+                    out=qg[:].rearrange("p (c i t) -> p c t i", i=4, t=4),
+                    in_=qp[:].rearrange("p (t c i) -> p c t i", t=4, i=4),
+                )
+            quantise(("z%d" % b, g2), qg)
+
+        sm = {}
+
+        def stage2(b, jh):
+            for n in range(4):
+                if jh == 0:
+                    sm[(b, n)] = soft.tile([P, 1024], F32, name="sm", tag="sm")
+                acc = ps_mm.tile([P, 512], F32, name="acc2", tag="mm")
+                for g2 in range(2):
+                    mx(
+                        acc[:], ("z%d" % b, g2), slice(128 * n, 128 * n + 128),
+                        ("c%d%d" % (b, jh), g2), slice(0, 512), g2 == 0, g2 == 1,
+                    )
+                s = sm[(b, n)]
+                nc.vector.scalar_tensor_tensor(
+                    out=s[:, 512 * jh : 512 * jh + 512],
+                    in0=cbm[:, 1024 * b + 512 * jh : 1024 * b + 512 * jh + 512],
+                    scalar=s10k[:, 4 * b + n : 4 * b + n + 1],
+                    in1=acc[:],
+                    op0=ALU.mult,
+                    op1=ALU.add,
+                )
+                if jh == 1:
+                    nmx = small.tile([P, 1], F32, name="nmx", tag="nmx")
+                    nc.vector.tensor_reduce(out=nmx[:], in_=s[:], axis=AX.X, op=ALU.max, negate=True)
+                    ssum = small.tile([P, 1], F32, name="ssum", tag="ssum")
+                    nc.scalar.activation(out=s[:], in_=s[:], func=ACT.Exp, bias=nmx[:], scale=1.0, accum_out=ssum[:])
+                    rs = small.tile([P, 1], F32, name="rs", tag="rs")
+                    nc.vector.reciprocal(rs[:], ssum[:])
+                    if NORM[b] == "S":
+                        nc.scalar.activation(out=s[:], in_=s[:], func=ACT.Copy, scale=rs[:])
+                    elif NORM[b] == "V":
+                        nc.vector.tensor_scalar(out=s[:], in0=s[:], scalar1=rs[:], scalar2=None, op0=ALU.mult)
+                    else:
+                        nc.gpsimd.tensor_scalar(out=s[:], in0=s[:], scalar1=rs[:], scalar2=0.0, op0=ALU.mult, op1=ALU.add)
+                    nc.sync.dma_start(out=out[b].rearrange("(p n) j -> p n j", n=4)[:, n, :], in_=s[:])
+
+        prep("q0", True)
+        prep("W0", True)
+        spread_mask()
+        prep("W1", True)
+        prep("c00", False)
+        prep("c01", False)
+        prep("q1", False)
+        prep("c10", False)
+        prep("c11", False)
+        stage1(0, 0)
+        stage1(0, 1)
+        stage2(0, 0)
+        stage1(1, 0)
+        stage1(1, 1)
+        stage2(0, 1)
+        stage2(1, 0)
+        stage2(1, 1)

@@ -15,10 +15,48 @@ AX = mybir.AxisListType
 P = 128
 FLOPS = 2 * 1024 * 1024 * 1024 + 2 * 2 * 512 * 1024 * 1024
 
-PIN = False
-ROUTE = {(0, 0): "S", (0, 1): "S", (1, 0): "S", (1, 1): "S"}
-NORM = {0: "G", 1: "G"}
-LOAD_ORDER = ["q0", "W0", "W1", "c00", "c01", "q1", "c10", "c11"]
+ROUTE = {(0, 0): "V", (0, 1): "V", (1, 0): "S", (1, 1): "S"}
+
+ORDER = [
+    ("L", "q0", 0), ("LB",), ("L", "q0", 1), ("L", "W0", 0), ("L", "W0", 1), ("L", "W1", 0),
+    ("L", "W1", 1), ("L", "c00", 0), ("L", "c00", 1), ("L", "c01", 0), ("L", "c01", 1), ("L", "q1", 0),
+    ("L", "q1", 1), ("L", "c10", 0), ("L", "c10", 1), ("L", "c11", 0), ("L", "c11", 1), ("BM", 1),
+    ("TP", "q0", 0, 0), ("BX", 1, "S"), ("TP", "q0", 1, 0), ("EX", "q0", 0, 0, "V"), ("TP", "q0", 0, 1), ("EX", "q0", 1, 0, "S"),
+    ("TP", "q0", 1, 1), ("EX", "q0", 0, 1, "V"), ("BM", 2), ("QZ", "q0", 0), ("TP", "W0", 1, 0), ("TP", "W0", 0, 0),
+    ("EX", "W0", 1, 0, "S"), ("EX", "q0", 1, 1, "V"), ("QZ", "q0", 1), ("TP", "W0", 1, 1), ("TP", "W0", 0, 1), ("EX", "W0", 1, 1, "S"),
+    ("EX", "W0", 0, 1, "V"), ("EX", "W0", 0, 0, "S"), ("TP", "W1", 0, 0), ("QZ", "W0", 1), ("BX", 2, "S"), ("TP", "W1", 1, 0),
+    ("QZ", "W0", 0), ("EX", "W1", 0, 0, "S"), ("TP", "W1", 1, 1), ("EX", "W1", 1, 0, "V"), ("TP", "W1", 0, 1), ("EX", "W1", 1, 1, "S"),
+    ("CB",), ("M1", 0, 0, 0), ("EX", "W1", 0, 1, "V"), ("M1", 0, 0, 2), ("QZ", "W1", 0), ("X1", 0, 0, 0),
+    ("TP", "c00", 0, 0), ("TP", "c00", 1, 0), ("EX", "c00", 0, 0, "S"), ("QZ2", 0, 0, 0), ("X1", 0, 0, 2), ("TP", "c00", 0, 1),
+    ("TP", "c00", 1, 1), ("EX", "c00", 1, 0, "S"), ("QZ", "W1", 1), ("M1", 0, 0, 3), ("EX", "c00", 1, 1, "S"), ("QZ2", 0, 0, 2),
+    ("M1", 0, 0, 1), ("X1", 0, 0, 3), ("EX", "c00", 0, 1, "S"), ("M1", 0, 1, 2), ("X1", 0, 0, 1), ("X1", 0, 1, 2),
+    ("TP", "c01", 0, 1), ("BM", 0), ("EX", "c01", 0, 1, "S"), ("QZ", "c00", 1), ("TP", "c01", 0, 0), ("TP", "q1", 0, 0),
+    ("EX", "c01", 0, 0, "S"), ("QZ", "c00", 0), ("TP", "c01", 1, 0), ("TP", "c01", 1, 1), ("EX", "q1", 0, 0, "S"), ("QZ2", 0, 0, 1),
+    ("QZ2", 0, 1, 2), ("QZ", "c01", 0), ("M1", 0, 1, 3), ("EX", "c01", 1, 1, "S"), ("QZ2", 0, 0, 3), ("M1", 0, 1, 0),
+    ("EX", "c01", 1, 0, "S"), ("X1", 0, 1, 3), ("M1", 0, 1, 1), ("BX", 0, "S"), ("X1", 0, 1, 0), ("QZ2", 0, 1, 3),
+    ("TP", "q1", 0, 1), ("X1", 0, 1, 1), ("TP", "q1", 1, 1), ("EX", "q1", 0, 1, "S"), ("TP", "q1", 1, 0), ("QZ2", 0, 1, 1),
+    ("QZ", "c01", 1), ("TP", "c10", 1, 1), ("EX", "q1", 1, 1, "S"), ("TP", "c10", 1, 0), ("QZ2", 0, 1, 0), ("EX", "q1", 1, 0, "S"),
+    ("QZ", "q1", 0), ("TP", "c11", 1, 0), ("CS",), ("M2", 0, 2, 1), ("EX", "c10", 1, 0, "S"), ("QZ", "q1", 1),
+    ("M2", 0, 2, 0), ("EX", "c11", 1, 0, "S"), ("D", 0, 2, 1), ("M2", 0, 0, 0), ("EX", "c10", 1, 1, "S"), ("D", 0, 2, 0),
+    ("M2", 0, 1, 1), ("D", 0, 0, 0), ("TP", "c11", 0, 0), ("QZ", "c10", 1), ("TP", "c10", 0, 0), ("EX", "c11", 0, 0, "S"),
+    ("TP", "c11", 0, 1), ("D", 0, 1, 1), ("TP", "c11", 1, 1), ("E", 0, 2), ("EX", "c11", 1, 1, "S"), ("M2", 0, 3, 1),
+    ("M2", 0, 1, 0), ("EX", "c10", 0, 0, "S"), ("D", 0, 3, 1), ("M1", 1, 0, 2), ("F", 0, 2), ("D", 0, 1, 0),
+    ("TP", "c10", 0, 1), ("BM", 3), ("QZ", "c11", 1), ("X1", 1, 0, 2), ("M2", 0, 0, 1), ("E", 0, 1),
+    ("BX", 3, "S"), ("M1", 1, 0, 3), ("EX", "c10", 0, 1, "S"), ("M1", 1, 0, 1), ("D", 0, 0, 1), ("X1", 1, 0, 3),
+    ("M2", 0, 3, 0), ("QZ", "c10", 0), ("X1", 1, 0, 1), ("M1", 1, 0, 0), ("D", 0, 3, 0), ("M1", 1, 1, 3),
+    ("X1", 1, 0, 0), ("E", 0, 3), ("M1", 1, 1, 0), ("X1", 1, 1, 3), ("M1", 1, 1, 2), ("X1", 1, 1, 0),
+    ("R", 0, 2), ("RG", 1, 0, "V"), ("M1", 1, 1, 1), ("X1", 1, 1, 2), ("X1", 1, 1, 1), ("QZ2", 1, 0),
+    ("EX", "c11", 0, 1, "S"), ("RG", 1, 1, "V"), ("F", 0, 1), ("QZ", "c11", 0), ("F", 0, 3), ("QZ2", 1, 1),
+    ("R", 0, 1), ("E", 0, 0), ("G", 0, 1, "P"), ("M2", 1, 0, 0), ("G", 0, 2, "S"), ("M2", 1, 0, 1),
+    ("D", 1, 0, 0), ("ST", 0, 1), ("M2", 1, 3, 0), ("F", 0, 0), ("D", 1, 0, 1), ("M2", 1, 1, 1),
+    ("R", 0, 3), ("E", 1, 0), ("M2", 1, 2, 0), ("G", 0, 3, "S"), ("M2", 1, 3, 1), ("D", 1, 3, 0),
+    ("F", 1, 0), ("ST", 0, 3), ("ST", 0, 2), ("D", 1, 1, 1), ("M2", 1, 1, 0), ("R", 0, 0),
+    ("D", 1, 3, 1), ("M2", 1, 2, 1), ("G", 0, 0, "S"), ("R", 1, 0), ("D", 1, 1, 0), ("G", 1, 0, "S"),
+    ("E", 1, 1), ("ST", 0, 0), ("D", 1, 2, 0), ("ST", 1, 0), ("F", 1, 1), ("E", 1, 3),
+    ("R", 1, 1), ("D", 1, 2, 1), ("F", 1, 3), ("G", 1, 1, "P"), ("E", 1, 2), ("ST", 1, 1),
+    ("R", 1, 3), ("G", 1, 3, "V"), ("F", 1, 2), ("ST", 1, 3), ("R", 1, 2), ("G", 1, 2, "V"),
+    ("ST", 1, 2),
+]
 
 
 def tile_attention_pa_kernel(tc, query, context, query_bit, context_bit, W_in, b_in, out):
@@ -27,13 +65,12 @@ def tile_attention_pa_kernel(tc, query, context, query_bit, context_bit, W_in, b
         const = ctx.enter_context(tc.tile_pool(name="const", bufs=1))
         raw = ctx.enter_context(tc.tile_pool(name="raw", bufs=1))
         keep = ctx.enter_context(tc.tile_pool(name="keep", bufs=1))
-        stage = ctx.enter_context(tc.tile_pool(name="stage", bufs=4))
+        stage = ctx.enter_context(tc.tile_pool(name="stage", bufs=8))
         soft = ctx.enter_context(tc.tile_pool(name="soft", bufs=8))
         small = ctx.enter_context(tc.tile_pool(name="small", bufs=8))
         ps_tp = ctx.enter_context(tc.psum_pool(name="ps_tp", bufs=4))
         ps_mm = ctx.enter_context(tc.psum_pool(name="ps_mm", bufs=4))
-        if PIN:
-            ctx.enter_context(tc.manual_schedule())
+        ctx.enter_context(tc.manual_schedule())
 
         bits = const.tile([P, 2048], BF16, name="bits")
         nc.vector.memset(bits[:], 0.0)
@@ -41,67 +78,30 @@ def tile_attention_pa_kernel(tc, query, context, query_bit, context_bit, W_in, b
         nc.vector.memset(ones[:], 1.0)
         qb_raw = const.tile([P, 8], BF16, name="qb_raw")
         b_raw = const.tile([P, 8], BF16, name="b_raw")
-
-        def small_loads():
-            nc.sync.dma_start(
-                out=b_raw[:].rearrange("p (k e) -> p k e", k=4),
-                in_=b_in.rearrange("(k p e) -> p k e", k=4, e=2),
-            )
-            nc.sync.dma_start(out=bits[0:1, :], in_=context_bit.rearrange("(o b) j -> o (b j)", o=1))
-            nc.sync.dma_start(
-                out=qb_raw[:].rearrange("p (b n) -> p b n", b=2),
-                in_=query_bit.rearrange("b (p n) -> p b n", n=4),
-            )
-
+        s10k = const.tile([P, 8], F32, name="s10k")
+        bias_f = const.tile([P, 8], F32, name="bias_f")
+        cbm = const.tile([P, 2048], BF16, name="cbm")
         ident = const.tile([P, P], F32, name="ident")
         make_identity(nc, ident[:])
 
         rawt = {}
-        for x in LOAD_ORDER:
-            rawt[x] = raw.tile([P, 4096], BF16, name="raw_" + x)
-            for a2 in range(2):
-                if x[0] == "q":
-                    src = query[int(x[1])].rearrange("(p n) d -> p n d", n=4)[:, 2 * a2 : 2 * a2 + 2, :]
-                elif x[0] == "W":
-                    blk = 2 * int(x[1]) + a2
-                    src = W_in[256 * blk : 256 * blk + 256, :].rearrange("(p e) d -> p e d", e=2)
-                else:
-                    r0 = 512 * int(x[2]) + 256 * a2
-                    src = context[int(x[1]), r0 : r0 + 256, :].rearrange("(c p) e -> p c e", p=P)
-                nc.sync.dma_start(
-                    out=rawt[x][:, 2048 * a2 : 2048 * a2 + 2048].rearrange("p (n d) -> p n d", n=2), in_=src
-                )
-            if x == "W0":
-                small_loads()
-
-        s10k = const.tile([P, 8], F32, name="s10k")
-        nc.vector.tensor_scalar(out=s10k[:], in0=qb_raw[:], scalar1=10000.0, scalar2=None, op0=ALU.mult)
-        bias_f = const.tile([P, 8], F32, name="bias_f")
-        nc.vector.tensor_copy(out=bias_f[:], in_=b_raw[:])
-
-        cbm = const.tile([P, 2048], BF16, name="cbm")
-
-        def spread_mask():
-          for c4 in range(4):
-            pb = ps_mm.tile([P, 512], F32, name="pb", tag="mm")
-            nc.tensor.matmul(out=pb[:], lhsT=ones[:], rhs=bits[:, 512 * c4 : 512 * c4 + 512], start=True, stop=True)
-            if c4 % 2 == 0:
-                nc.vector.tensor_scalar(
-                    out=cbm[:, 512 * c4 : 512 * c4 + 512], in0=pb[:], scalar1=-1.0, scalar2=None, op0=ALU.add
-                )
-            else:
-                nc.scalar.activation(out=cbm[:, 512 * c4 : 512 * c4 + 512], in_=pb[:], func=ACT.Copy, bias=-1.0, scale=1.0)
-
         codes = {}
         scales = {}
+        bank = {}
+        grp = {}
+        sm = {}
+        tiny = {}
 
-        def new_codes(key):
-            codes[key] = keep.tile([P, 512], U32, name="c_%s_%d" % key, align_bytes=64)
-            scales[key] = keep.tile([P, 512], U8, name="s_%s_%d" % key, align_bytes=64)
+        def copy_out(eng, dst, src):
+            if eng == "V":
+                nc.vector.tensor_copy(out=dst, in_=src)
+            else:
+                nc.scalar.copy(out=dst, in_=src)
 
-        def quantise(key, grouped):
-            new_codes(key)
-            nc.vector.quantize_mx(out=codes[key][:].bitcast(FP8X4), scales=scales[key][:], in_=grouped[:])
+        def quantise(key, width, grouped):
+            codes[key] = keep.tile([P, width], U32, name="c_%s_%d_%d" % key, align_bytes=64)
+            scales[key] = keep.tile([P, width], U8, name="s_%s_%d_%d" % key, align_bytes=64)
+            nc.vector.quantize_mx(out=codes[key][:].bitcast(FP8X4), scales=scales[key][:], in_=grouped)
 
         def mx(acc, wkey, wcols, mkey, mcols, start, stop):
             nc.tensor.matmul_mx(
@@ -114,115 +114,174 @@ def tile_attention_pa_kernel(tc, query, context, query_bit, context_bit, W_in, b
                 stop=stop,
             )
 
-        def prep(x, early):
-            words = rawt[x][:].bitcast(F32)
-            for g in range(2):
-                grouped = stage.tile([P, 2048], BF16, name="grp", tag="grp", align_bytes=64)
-                for a2 in range(2):
-                    tp = ps_tp.tile([P, 512], F32, name="tp", tag="tp")
-                    for a in range(2):
-                        for u in range(2):
-                            col = (2 * a2 + a) * 512 + g * 256 + u * 128
-                            nc.tensor.transpose(
-                                tp[:, (2 * a + u) * 128 : (2 * a + u) * 128 + 128], words[:, col : col + 128], ident[:]
-                            )
-                    dst = grouped[:].bitcast(F32)[:, 512 * a2 : 512 * a2 + 512].rearrange(
-                        "p (a r u) -> p a r u", a=2, u=2
-                    )
-                    srcv = tp[:].rearrange("p (a u r) -> p a r u", a=2, u=2)
-                    if early and a2 == 1:
-                        nc.vector.tensor_copy(out=dst, in_=srcv)
-                    else:
-                        nc.scalar.copy(out=dst, in_=srcv)
-                quantise((x, g), grouped)
+        def do_L(x, a2):
+            if a2 == 0:
+                rawt[x] = raw.tile([P, 4096], BF16, name="raw_" + x)
+            if x[0] == "q":
+                src = query[int(x[1])].rearrange("(p n) d -> p n d", n=4)[:, 2 * a2 : 2 * a2 + 2, :]
+            elif x[0] == "W":
+                blk = 2 * int(x[1]) + a2
+                src = W_in[256 * blk : 256 * blk + 256, :].rearrange("(p e) d -> p e d", e=2)
+            else:
+                r0 = 512 * int(x[2]) + 256 * a2
+                src = context[int(x[1]), r0 : r0 + 256, :].rearrange("(c p) e -> p c e", p=P)
+            nc.sync.dma_start(out=rawt[x][:, 2048 * a2 : 2048 * a2 + 2048].rearrange("p (n d) -> p n d", n=2), in_=src)
+            if x == "W0" and a2 == 1:
+                nc.sync.dma_start(
+                    out=b_raw[:].rearrange("p (k e) -> p k e", k=4), in_=b_in.rearrange("(k p e) -> p k e", k=4, e=2)
+                )
+                nc.sync.dma_start(
+                    out=qb_raw[:].rearrange("p (b n) -> p b n", b=2), in_=query_bit.rearrange("b (p n) -> p b n", n=4)
+                )
 
-        def stage1(b, g2):
-            qg = stage.tile([P, 2048], BF16, name="qg", tag="qg", bufs=2, align_bytes=64)
+        def do_CB():
+            nc.vector.tensor_copy(out=bias_f[:], in_=b_raw[:])
+
+        def do_CS():
+            nc.vector.tensor_scalar(out=s10k[:], in0=qb_raw[:], scalar1=10000.0, scalar2=None, op0=ALU.mult)
+
+        def do_LB():
+            nc.sync.dma_start(out=bits[0:1, :], in_=context_bit.rearrange("(o b) j -> o (b j)", o=1))
+
+        def do_BM(c4):
+            bank[("B", c4)] = ps_mm.tile([P, 512], F32, name="pb", tag="mm")
+            nc.tensor.matmul(
+                out=bank[("B", c4)][:], lhsT=ones[:], rhs=bits[:, 512 * c4 : 512 * c4 + 512], start=True, stop=True
+            )
+
+        def do_BX(c4, eng):
+            dst = cbm[:, 512 * c4 : 512 * c4 + 512]
+            if eng == "V":
+                nc.vector.tensor_scalar(out=dst, in0=bank[("B", c4)][:], scalar1=-1.0, scalar2=None, op0=ALU.add)
+            else:
+                nc.scalar.activation(out=dst, in_=bank[("B", c4)][:], func=ACT.Copy, bias=-1.0, scale=1.0)
+
+        def do_TP(x, g, a2):
+            words = rawt[x][:].bitcast(F32)
+            tp = ps_tp.tile([P, 512], F32, name="tp", tag="tp")
+            bank[("T", x, g, a2)] = tp
+            for a in range(2):
+                for u in range(2):
+                    col = (2 * a2 + a) * 512 + g * 256 + u * 128
+                    nc.tensor.transpose(
+                        tp[:, (2 * a + u) * 128 : (2 * a + u) * 128 + 128], words[:, col : col + 128], ident[:]
+                    )
+
+        def do_EX(x, g, a2, eng):
+            if (x, g) not in grp:
+                grp[(x, g)] = stage.tile([P, 2048], BF16, name="grp", tag="grp", align_bytes=64)
+            dst = grp[(x, g)][:].bitcast(F32)[:, 512 * a2 : 512 * a2 + 512].rearrange("p (a r u) -> p a r u", a=2, u=2)
+            copy_out(eng, dst, bank[("T", x, g, a2)][:].rearrange("p (a u r) -> p a r u", a=2, u=2))
+
+        def do_QZ(x, g):
+            quantise((x, g, 0), 512, grp[(x, g)][:])
+
+        def do_M1(b, g2, n):
+            acc = ps_mm.tile([P, 512], F32, name="acc1", tag="mm")
+            bank[("1", b, g2, n)] = acc
             wx = "W%d" % g2
             qx = "q%d" % b
             if ROUTE[(b, g2)] == "V":
-                for n in range(4):
-                    acc = ps_mm.tile([P, 512], F32, name="acc1", tag="mm")
-                    for t in range(4):
-                        for g in range(2):
-                            mx(
-                                acc[:, 128 * t : 128 * t + 128],
-                                (wx, g), slice(128 * t, 128 * t + 128),
-                                (qx, g), slice(128 * n, 128 * n + 128),
-                                g == 0, g == 1,
-                            )
-                    nc.vector.tensor_tensor(
-                        out=qg[:, 512 * n : 512 * n + 512].rearrange("p (i t) -> p i t", t=4),
-                        in0=acc[:].rearrange("p (t i) -> p i t", t=4),
-                        in1=bias_f[:, 4 * g2 : 4 * g2 + 4].unsqueeze(1).to_broadcast([P, 128, 4]),
-                        op=ALU.add,
-                    )
-            else:
-                qp = stage.tile([P, 2048], BF16, name="qp", tag="qp", bufs=2)
                 for t in range(4):
-                    acc = ps_mm.tile([P, 512], F32, name="acc1", tag="mm")
                     for g in range(2):
-                        mx(acc[:], (wx, g), slice(128 * t, 128 * t + 128), (qx, g), slice(0, 512), g == 0, g == 1)
-                    nc.scalar.activation(
-                        out=qp[:, 512 * t : 512 * t + 512], in_=acc[:], func=ACT.Identity,
-                        bias=bias_f[:, 4 * g2 + t : 4 * g2 + t + 1], scale=1.0,
-                    )
-                nc.vector.tensor_copy(
-                    out=qg[:].rearrange("p (c i t) -> p c t i", i=4, t=4),
-                    in_=qp[:].rearrange("p (t c i) -> p c t i", t=4, i=4),
+                        mx(
+                            acc[:, 128 * t : 128 * t + 128],
+                            (wx, g, 0), slice(128 * t, 128 * t + 128),
+                            (qx, g, 0), slice(128 * n, 128 * n + 128),
+                            g == 0, g == 1,
+                        )
+            else:
+                for g in range(2):
+                    mx(acc[:], (wx, g, 0), slice(128 * n, 128 * n + 128), (qx, g, 0), slice(0, 512), g == 0, g == 1)
+
+        def do_X1(b, g2, n):
+            acc = bank[("1", b, g2, n)]
+            if ROUTE[(b, g2)] == "V":
+                if ("g", b, g2) not in grp:
+                    grp[("g", b, g2)] = stage.tile([P, 2048], BF16, name="qg", tag="qg", bufs=4, align_bytes=64)
+                nc.vector.tensor_tensor(
+                    out=grp[("g", b, g2)][:, 512 * n : 512 * n + 512].rearrange("p (i t) -> p i t", t=4),
+                    in0=acc[:].rearrange("p (t i) -> p i t", t=4),
+                    in1=bias_f[:, 4 * g2 : 4 * g2 + 4].unsqueeze(1).to_broadcast([P, 128, 4]),
+                    op=ALU.add,
                 )
-            quantise(("z%d" % b, g2), qg)
-
-        sm = {}
-
-        def stage2(b, jh):
-            for n in range(4):
-                if jh == 0:
-                    sm[(b, n)] = soft.tile([P, 1024], F32, name="sm", tag="sm")
-                acc = ps_mm.tile([P, 512], F32, name="acc2", tag="mm")
-                for g2 in range(2):
-                    mx(
-                        acc[:], ("z%d" % b, g2), slice(128 * n, 128 * n + 128),
-                        ("c%d%d" % (b, jh), g2), slice(0, 512), g2 == 0, g2 == 1,
-                    )
-                s = sm[(b, n)]
-                nc.vector.scalar_tensor_tensor(
-                    out=s[:, 512 * jh : 512 * jh + 512],
-                    in0=cbm[:, 1024 * b + 512 * jh : 1024 * b + 512 * jh + 512],
-                    scalar=s10k[:, 4 * b + n : 4 * b + n + 1],
-                    in1=acc[:],
-                    op0=ALU.mult,
-                    op1=ALU.add,
+            else:
+                if ("p", b, g2) not in grp:
+                    grp[("p", b, g2)] = stage.tile([P, 2048], BF16, name="qp", tag="qp", bufs=2)
+                nc.scalar.activation(
+                    out=grp[("p", b, g2)][:, 512 * n : 512 * n + 512], in_=acc[:], func=ACT.Identity,
+                    bias=bias_f[:, 4 * g2 + n : 4 * g2 + n + 1], scale=1.0,
                 )
-                if jh == 1:
-                    nmx = small.tile([P, 1], F32, name="nmx", tag="nmx")
-                    nc.vector.tensor_reduce(out=nmx[:], in_=s[:], axis=AX.X, op=ALU.max, negate=True)
-                    ssum = small.tile([P, 1], F32, name="ssum", tag="ssum")
-                    nc.scalar.activation(out=s[:], in_=s[:], func=ACT.Exp, bias=nmx[:], scale=1.0, accum_out=ssum[:])
-                    rs = small.tile([P, 1], F32, name="rs", tag="rs")
-                    nc.vector.reciprocal(rs[:], ssum[:])
-                    if NORM[b] == "S":
-                        nc.scalar.activation(out=s[:], in_=s[:], func=ACT.Copy, scale=rs[:])
-                    elif NORM[b] == "V":
-                        nc.vector.tensor_scalar(out=s[:], in0=s[:], scalar1=rs[:], scalar2=None, op0=ALU.mult)
-                    else:
-                        nc.gpsimd.tensor_scalar(out=s[:], in0=s[:], scalar1=rs[:], scalar2=0.0, op0=ALU.mult, op1=ALU.add)
-                    nc.sync.dma_start(out=out[b].rearrange("(p n) j -> p n j", n=4)[:, n, :], in_=s[:])
 
-        prep("q0", True)
-        prep("W0", True)
-        spread_mask()
-        prep("W1", True)
-        prep("c00", False)
-        prep("c01", False)
-        prep("q1", False)
-        prep("c10", False)
-        prep("c11", False)
-        stage1(0, 0)
-        stage1(0, 1)
-        stage2(0, 0)
-        stage1(1, 0)
-        stage1(1, 1)
-        stage2(0, 1)
-        stage2(1, 0)
-        stage2(1, 1)
+        def do_RG(b, g2, eng):
+            grp[("g", b, g2)] = stage.tile([P, 2048], BF16, name="qg", tag="qg", bufs=4, align_bytes=64)
+            dst = grp[("g", b, g2)][:].rearrange("p (c i t) -> p c t i", i=4, t=4)
+            src = grp[("p", b, g2)][:].rearrange("p (t c i) -> p c t i", t=4, i=4)
+            if eng == "V":
+                nc.vector.tensor_copy(out=dst, in_=src)
+            else:
+                nc.gpsimd.tensor_scalar(out=dst, in0=src, scalar1=1.0, scalar2=0.0, op0=ALU.mult, op1=ALU.add)
+
+        def do_QZ2(b, g2, n=None):
+            if n is None:
+                quantise(("z%d" % b, g2, 0), 512, grp[("g", b, g2)][:])
+            else:
+                quantise(("z%d" % b, g2, n), 128, grp[("g", b, g2)][:, 512 * n : 512 * n + 512])
+
+        def do_M2(b, n, jh):
+            acc = ps_mm.tile([P, 512], F32, name="acc2", tag="mm")
+            bank[("2", b, n, jh)] = acc
+            for g2 in range(2):
+                if ROUTE[(b, g2)] == "V":
+                    wkey, wcols = ("z%d" % b, g2, n), slice(0, 128)
+                else:
+                    wkey, wcols = ("z%d" % b, g2, 0), slice(128 * n, 128 * n + 128)
+                mx(acc[:], wkey, wcols, ("c%d%d" % (b, jh), g2, 0), slice(0, 512), g2 == 0, g2 == 1)
+
+        def do_D(b, n, jh):
+            if (b, n) not in sm:
+                sm[(b, n)] = soft.tile([P, 1024], F32, name="sm", tag="sm")
+            nc.vector.scalar_tensor_tensor(
+                out=sm[(b, n)][:, 512 * jh : 512 * jh + 512],
+                in0=cbm[:, 1024 * b + 512 * jh : 1024 * b + 512 * jh + 512],
+                scalar=s10k[:, 4 * b + n : 4 * b + n + 1],
+                in1=bank[("2", b, n, jh)][:],
+                op0=ALU.mult,
+                op1=ALU.add,
+            )
+
+        def do_E(b, n):
+            tiny[("m", b, n)] = small.tile([P, 1], F32, name="nmx", tag="nmx")
+            nc.vector.tensor_reduce(out=tiny[("m", b, n)][:], in_=sm[(b, n)][:], axis=AX.X, op=ALU.max, negate=True)
+
+        def do_F(b, n):
+            tiny[("s", b, n)] = small.tile([P, 1], F32, name="ssum", tag="ssum")
+            s = sm[(b, n)]
+            nc.scalar.activation(
+                out=s[:], in_=s[:], func=ACT.Exp, bias=tiny[("m", b, n)][:], scale=1.0, accum_out=tiny[("s", b, n)][:]
+            )
+
+        def do_R(b, n):
+            tiny[("r", b, n)] = small.tile([P, 1], F32, name="rs", tag="rs")
+            nc.vector.reciprocal(tiny[("r", b, n)][:], tiny[("s", b, n)][:])
+
+        def do_G(b, n, eng):
+            s = sm[(b, n)]
+            rs = tiny[("r", b, n)]
+            if eng == "S":
+                nc.scalar.activation(out=s[:], in_=s[:], func=ACT.Copy, scale=rs[:])
+            elif eng == "V":
+                nc.vector.tensor_scalar(out=s[:], in0=s[:], scalar1=rs[:], scalar2=None, op0=ALU.mult)
+            else:
+                nc.gpsimd.tensor_scalar(out=s[:], in0=s[:], scalar1=rs[:], scalar2=0.0, op0=ALU.mult, op1=ALU.add)
+
+        def do_ST(b, n):
+            nc.sync.dma_start(out=out[b].rearrange("(p n) j -> p n j", n=4)[:, n, :], in_=sm[(b, n)][:])
+
+        table = {
+            "L": do_L, "LB": do_LB, "BM": do_BM, "BX": do_BX, "TP": do_TP, "EX": do_EX, "QZ": do_QZ, "M1": do_M1,
+            "X1": do_X1, "RG": do_RG, "QZ2": do_QZ2, "M2": do_M2, "D": do_D, "E": do_E, "F": do_F, "R": do_R,
+            "G": do_G, "ST": do_ST, "CB": do_CB, "CS": do_CS,
+        }
+        for step in ORDER:
+            table[step[0]](*step[1:])

@@ -15,47 +15,49 @@ AX = mybir.AxisListType
 P = 128
 FLOPS = 2 * 1024 * 1024 * 1024 + 2 * 2 * 512 * 1024 * 1024
 
-ROUTE = {(0, 0): "V", (0, 1): "V", (1, 0): "S", (1, 1): "S"}
+ROUTE = {(0, 0): "S", (0, 1): "S", (1, 0): "S", (1, 1): "S"}
+
+RG_HALVES = True
 
 ORDER = [
     ("L", "q0", 0), ("LB",), ("L", "q0", 1), ("L", "W0", 0), ("L", "W0", 1), ("L", "W1", 0),
     ("L", "W1", 1), ("L", "c00", 0), ("L", "c00", 1), ("L", "c01", 0), ("L", "c01", 1), ("L", "q1", 0),
-    ("L", "q1", 1), ("L", "c10", 0), ("L", "c10", 1), ("L", "c11", 0), ("L", "c11", 1), ("BM", 1),
-    ("TP", "q0", 0, 0), ("BX", 1, "S"), ("TP", "q0", 1, 0), ("EX", "q0", 0, 0, "V"), ("TP", "q0", 0, 1), ("EX", "q0", 1, 0, "S"),
-    ("TP", "q0", 1, 1), ("EX", "q0", 0, 1, "V"), ("BM", 2), ("QZ", "q0", 0), ("TP", "W0", 1, 0), ("TP", "W0", 0, 0),
-    ("EX", "W0", 1, 0, "S"), ("EX", "q0", 1, 1, "V"), ("QZ", "q0", 1), ("TP", "W0", 1, 1), ("TP", "W0", 0, 1), ("EX", "W0", 1, 1, "S"),
-    ("EX", "W0", 0, 1, "V"), ("EX", "W0", 0, 0, "S"), ("TP", "W1", 0, 0), ("QZ", "W0", 1), ("BX", 2, "S"), ("TP", "W1", 1, 0),
-    ("QZ", "W0", 0), ("EX", "W1", 0, 0, "S"), ("TP", "W1", 1, 1), ("EX", "W1", 1, 0, "V"), ("TP", "W1", 0, 1), ("EX", "W1", 1, 1, "S"),
-    ("CB",), ("M1", 0, 0, 0), ("EX", "W1", 0, 1, "V"), ("M1", 0, 0, 2), ("QZ", "W1", 0), ("X1", 0, 0, 0),
-    ("TP", "c00", 0, 0), ("TP", "c00", 1, 0), ("EX", "c00", 0, 0, "S"), ("QZ2", 0, 0, 0), ("X1", 0, 0, 2), ("TP", "c00", 0, 1),
-    ("TP", "c00", 1, 1), ("EX", "c00", 1, 0, "S"), ("QZ", "W1", 1), ("M1", 0, 0, 3), ("EX", "c00", 1, 1, "S"), ("QZ2", 0, 0, 2),
-    ("M1", 0, 0, 1), ("X1", 0, 0, 3), ("EX", "c00", 0, 1, "S"), ("M1", 0, 1, 2), ("X1", 0, 0, 1), ("X1", 0, 1, 2),
-    ("TP", "c01", 0, 1), ("BM", 0), ("EX", "c01", 0, 1, "S"), ("QZ", "c00", 1), ("TP", "c01", 0, 0), ("TP", "q1", 0, 0),
-    ("EX", "c01", 0, 0, "S"), ("QZ", "c00", 0), ("TP", "c01", 1, 0), ("TP", "c01", 1, 1), ("EX", "q1", 0, 0, "S"), ("QZ2", 0, 0, 1),
-    ("QZ2", 0, 1, 2), ("QZ", "c01", 0), ("M1", 0, 1, 3), ("EX", "c01", 1, 1, "S"), ("QZ2", 0, 0, 3), ("M1", 0, 1, 0),
-    ("EX", "c01", 1, 0, "S"), ("X1", 0, 1, 3), ("M1", 0, 1, 1), ("BX", 0, "S"), ("X1", 0, 1, 0), ("QZ2", 0, 1, 3),
-    ("TP", "q1", 0, 1), ("X1", 0, 1, 1), ("TP", "q1", 1, 1), ("EX", "q1", 0, 1, "S"), ("TP", "q1", 1, 0), ("QZ2", 0, 1, 1),
-    ("QZ", "c01", 1), ("TP", "c10", 1, 1), ("EX", "q1", 1, 1, "S"), ("TP", "c10", 1, 0), ("QZ2", 0, 1, 0), ("EX", "q1", 1, 0, "S"),
-    ("QZ", "q1", 0), ("TP", "c11", 1, 0), ("CS",), ("M2", 0, 2, 1), ("EX", "c10", 1, 0, "S"), ("QZ", "q1", 1),
-    ("M2", 0, 2, 0), ("EX", "c11", 1, 0, "S"), ("D", 0, 2, 1), ("M2", 0, 0, 0), ("EX", "c10", 1, 1, "S"), ("D", 0, 2, 0),
-    ("M2", 0, 1, 1), ("D", 0, 0, 0), ("TP", "c11", 0, 0), ("QZ", "c10", 1), ("TP", "c10", 0, 0), ("EX", "c11", 0, 0, "S"),
-    ("TP", "c11", 0, 1), ("D", 0, 1, 1), ("TP", "c11", 1, 1), ("E", 0, 2), ("EX", "c11", 1, 1, "S"), ("M2", 0, 3, 1),
-    ("M2", 0, 1, 0), ("EX", "c10", 0, 0, "S"), ("D", 0, 3, 1), ("M1", 1, 0, 2), ("F", 0, 2), ("D", 0, 1, 0),
-    ("TP", "c10", 0, 1), ("BM", 3), ("QZ", "c11", 1), ("X1", 1, 0, 2), ("M2", 0, 0, 1), ("E", 0, 1),
-    ("BX", 3, "S"), ("M1", 1, 0, 3), ("EX", "c10", 0, 1, "S"), ("M1", 1, 0, 1), ("D", 0, 0, 1), ("X1", 1, 0, 3),
-    ("M2", 0, 3, 0), ("QZ", "c10", 0), ("X1", 1, 0, 1), ("M1", 1, 0, 0), ("D", 0, 3, 0), ("M1", 1, 1, 3),
-    ("X1", 1, 0, 0), ("E", 0, 3), ("M1", 1, 1, 0), ("X1", 1, 1, 3), ("M1", 1, 1, 2), ("X1", 1, 1, 0),
-    ("R", 0, 2), ("RG", 1, 0, "V"), ("M1", 1, 1, 1), ("X1", 1, 1, 2), ("X1", 1, 1, 1), ("QZ2", 1, 0),
-    ("EX", "c11", 0, 1, "S"), ("RG", 1, 1, "V"), ("F", 0, 1), ("QZ", "c11", 0), ("F", 0, 3), ("QZ2", 1, 1),
-    ("R", 0, 1), ("E", 0, 0), ("G", 0, 1, "P"), ("M2", 1, 0, 0), ("G", 0, 2, "S"), ("M2", 1, 0, 1),
-    ("D", 1, 0, 0), ("ST", 0, 1), ("M2", 1, 3, 0), ("F", 0, 0), ("D", 1, 0, 1), ("M2", 1, 1, 1),
-    ("R", 0, 3), ("E", 1, 0), ("M2", 1, 2, 0), ("G", 0, 3, "S"), ("M2", 1, 3, 1), ("D", 1, 3, 0),
-    ("F", 1, 0), ("ST", 0, 3), ("ST", 0, 2), ("D", 1, 1, 1), ("M2", 1, 1, 0), ("R", 0, 0),
-    ("D", 1, 3, 1), ("M2", 1, 2, 1), ("G", 0, 0, "S"), ("R", 1, 0), ("D", 1, 1, 0), ("G", 1, 0, "S"),
-    ("E", 1, 1), ("ST", 0, 0), ("D", 1, 2, 0), ("ST", 1, 0), ("F", 1, 1), ("E", 1, 3),
-    ("R", 1, 1), ("D", 1, 2, 1), ("F", 1, 3), ("G", 1, 1, "P"), ("E", 1, 2), ("ST", 1, 1),
-    ("R", 1, 3), ("G", 1, 3, "V"), ("F", 1, 2), ("ST", 1, 3), ("R", 1, 2), ("G", 1, 2, "V"),
-    ("ST", 1, 2),
+    ("L", "q1", 1), ("L", "c10", 0), ("L", "c10", 1), ("L", "c11", 0), ("L", "c11", 1), ("TP", "q0", 1, 0),
+    ("CM",), ("TP", "q0", 0, 0), ("EX", "q0", 1, 0, "S"), ("BM", 1), ("EX", "q0", 0, 0, "V"), ("TP", "q0", 1, 1),
+    ("BX", 1, "S"), ("TP", "q0", 0, 1), ("EX", "q0", 1, 1, "V"), ("EX", "q0", 0, 1, "S"), ("TP", "W0", 0, 0), ("QZ", "q0", 1),
+    ("TP", "W0", 1, 0), ("EX", "W0", 0, 0, "S"), ("QZ", "q0", 0), ("EX", "W0", 1, 0, "S"), ("TP", "W0", 0, 1), ("TP", "W0", 1, 1),
+    ("EX", "W0", 0, 1, "S"), ("BM", 0), ("EX", "W0", 1, 1, "S"), ("QZ", "W0", 0), ("TP", "W1", 1, 0), ("TP", "W1", 0, 0),
+    ("BX", 0, "S"), ("QZ", "W0", 1), ("TP", "W1", 0, 1), ("EX", "W1", 0, 0, "V"), ("TP", "W1", 1, 1), ("EX", "W1", 0, 1, "V"),
+    ("CB",), ("M1", 0, 0, 2), ("EX", "W1", 1, 0, "V"), ("M1", 0, 0, 3), ("X1", 0, 0, 2), ("M1", 0, 0, 0),
+    ("QZ", "W1", 0), ("X1", 0, 0, 3), ("M1", 0, 0, 1), ("EX", "W1", 1, 1, "V"), ("X1", 0, 0, 0), ("TP", "c00", 0, 0),
+    ("QZ", "W1", 1), ("X1", 0, 0, 1), ("TP", "c00", 0, 1), ("TP", "c01", 1, 0), ("EX", "c00", 0, 0, "V"), ("EX", "c00", 0, 1, "S"),
+    ("TP", "c01", 0, 0), ("RG", 0, 0, 0, "P"), ("EX", "c01", 1, 0, "V"), ("M1", 0, 1, 0), ("EX", "c01", 0, 0, "S"), ("QZ", "c00", 0),
+    ("M1", 0, 1, 3), ("X1", 0, 1, 0), ("RG", 0, 0, 1, "P"), ("M1", 0, 1, 1), ("QZ2", 0, 0, 0), ("X1", 0, 1, 3),
+    ("TP", "q1", 1, 0), ("X1", 0, 1, 1), ("TP", "c01", 1, 1), ("EX", "q1", 1, 0, "V"), ("TP", "q1", 0, 0), ("EX", "c01", 1, 1, "S"),
+    ("TP", "c01", 0, 1), ("QZ2", 0, 0, 1), ("M1", 0, 1, 2), ("EX", "q1", 0, 0, "S"), ("EX", "c01", 0, 1, "V"), ("TP", "c00", 1, 1),
+    ("QZ", "c01", 0), ("X1", 0, 1, 2), ("TP", "c10", 1, 0), ("QZ", "c01", 1), ("TP", "c00", 1, 0), ("EX", "c00", 1, 1, "S"),
+    ("RG", 0, 1, 0, "P"), ("TP", "q1", 1, 1), ("EX", "c00", 1, 0, "V"), ("EX", "c10", 1, 0, "S"), ("TP", "q1", 0, 1), ("QZ", "c00", 1),
+    ("EX", "q1", 1, 1, "S"), ("TP", "c10", 1, 1), ("RG", 0, 1, 1, "P"), ("EX", "q1", 0, 1, "S"), ("QZ2", 0, 1, 0), ("TP", "c11", 1, 0),
+    ("QZ", "q1", 1), ("TP", "c11", 0, 0), ("EX", "c10", 1, 1, "S"), ("CS",), ("M2", 0, 1, 0), ("QZ", "q1", 0),
+    ("EX", "c11", 1, 0, "S"), ("M2", 0, 1, 1), ("QZ2", 0, 1, 1), ("EX", "c11", 0, 0, "S"), ("D", 0, 1, 0), ("M1", 1, 0, 1),
+    ("D", 0, 1, 1), ("TP", "c11", 1, 1), ("TP", "c11", 0, 1), ("E", 0, 1), ("EX", "c11", 1, 1, "S"), ("M2", 0, 2, 0),
+    ("X1", 1, 0, 1), ("M1", 1, 0, 0), ("D", 0, 2, 0), ("EX", "c11", 0, 1, "S"), ("M1", 1, 1, 3), ("QZ", "c10", 1),
+    ("X1", 1, 0, 0), ("M2", 0, 2, 1), ("QZ", "c11", 0), ("X1", 1, 1, 3), ("M1", 1, 0, 2), ("D", 0, 2, 1),
+    ("M1", 1, 0, 3), ("X1", 1, 0, 2), ("QZ", "c11", 1), ("M1", 1, 1, 0), ("X1", 1, 0, 3), ("E", 0, 2),
+    ("M2", 0, 3, 1), ("X1", 1, 1, 0), ("RG", 1, 0, 0, "P"), ("M2", 0, 0, 1), ("F", 0, 1), ("M2", 0, 0, 0),
+    ("D", 0, 3, 1), ("M1", 1, 1, 1), ("D", 0, 0, 1), ("RG", 1, 0, 1, "P"), ("M1", 1, 1, 2), ("D", 0, 0, 0),
+    ("X1", 1, 1, 1), ("TP", "c10", 0, 0), ("QZ2", 1, 0, 0), ("X1", 1, 1, 2), ("TP", "c10", 0, 1), ("E", 0, 0),
+    ("EX", "c10", 0, 0, "S"), ("M2", 0, 3, 0), ("RG", 1, 1, 0, "P"), ("EX", "c10", 0, 1, "S"), ("D", 0, 3, 0), ("F", 0, 2),
+    ("E", 0, 3), ("RG", 1, 1, 1, "P"), ("QZ2", 1, 1, 0), ("F", 0, 3), ("R", 0, 2), ("R", 0, 1),
+    ("QZ", "c10", 0), ("G", 0, 1, "P"), ("M2", 1, 0, 1), ("QZ2", 1, 0, 1), ("M2", 1, 1, 1), ("F", 0, 0),
+    ("QZ2", 1, 1, 1), ("D", 1, 0, 1), ("G", 0, 2, "P"), ("M2", 1, 0, 0), ("ST", 0, 1), ("D", 1, 1, 1),
+    ("M2", 1, 1, 0), ("M2", 1, 3, 1), ("R", 0, 3), ("D", 1, 0, 0), ("G", 0, 3, "P"), ("M2", 1, 2, 0),
+    ("D", 1, 1, 0), ("M2", 1, 3, 0), ("R", 0, 0), ("E", 1, 0), ("G", 0, 0, "P"), ("M2", 1, 2, 1),
+    ("D", 1, 3, 0), ("F", 1, 0), ("ST", 0, 0), ("ST", 0, 2), ("E", 1, 1), ("R", 1, 0),
+    ("D", 1, 2, 1), ("F", 1, 1), ("G", 1, 0, "P"), ("D", 1, 2, 0), ("E", 1, 2), ("ST", 1, 0),
+    ("ST", 0, 3), ("R", 1, 1), ("D", 1, 3, 1), ("F", 1, 2), ("G", 1, 1, "P"), ("E", 1, 3),
+    ("ST", 1, 1), ("R", 1, 2), ("G", 1, 2, "V"), ("F", 1, 3), ("ST", 1, 2), ("R", 1, 3),
+    ("G", 1, 3, 1, "V"), ("G", 1, 3, 0, "V"), ("ST", 1, 3, 1), ("ST", 1, 3, 0),
 ]
 
 
@@ -74,6 +76,7 @@ def tile_attention_pa_kernel(tc, query, context, query_bit, context_bit, W_in, b
 
         bits = const.tile([P, 2048], BF16, name="bits")
         nc.vector.memset(bits[:], 0.0)
+        bits_raw = const.tile([1, 2048], BF16, name="bits_raw")
         ones = const.tile([P, P], BF16, name="ones")
         nc.vector.memset(ones[:], 1.0)
         qb_raw = const.tile([P, 8], BF16, name="qb_raw")
@@ -123,8 +126,8 @@ def tile_attention_pa_kernel(tc, query, context, query_bit, context_bit, W_in, b
                 blk = 2 * int(x[1]) + a2
                 src = W_in[256 * blk : 256 * blk + 256, :].rearrange("(p e) d -> p e d", e=2)
             else:
-                r0 = 512 * int(x[2]) + 256 * a2
-                src = context[int(x[1]), r0 : r0 + 256, :].rearrange("(c p) e -> p c e", p=P)
+                r0 = 512 * int(x[2])
+                src = context[int(x[1]), r0 : r0 + 512, :].rearrange("(p c) e -> p c e", c=4)[:, 2 * a2 : 2 * a2 + 2, :]
             nc.sync.dma_start(out=rawt[x][:, 2048 * a2 : 2048 * a2 + 2048].rearrange("p (n d) -> p n d", n=2), in_=src)
             if x == "W0" and a2 == 1:
                 nc.sync.dma_start(
@@ -141,20 +144,21 @@ def tile_attention_pa_kernel(tc, query, context, query_bit, context_bit, W_in, b
             nc.vector.tensor_scalar(out=s10k[:], in0=qb_raw[:], scalar1=10000.0, scalar2=None, op0=ALU.mult)
 
         def do_LB():
-            nc.sync.dma_start(out=bits[0:1, :], in_=context_bit.rearrange("(o b) j -> o (b j)", o=1))
+            nc.sync.dma_start(out=bits_raw[:], in_=context_bit.rearrange("(o b) j -> o (b j)", o=1))
 
-        def do_BM(c4):
-            bank[("B", c4)] = ps_mm.tile([P, 512], F32, name="pb", tag="mm")
-            nc.tensor.matmul(
-                out=bank[("B", c4)][:], lhsT=ones[:], rhs=bits[:, 512 * c4 : 512 * c4 + 512], start=True, stop=True
-            )
+        def do_CM():
+            nc.vector.tensor_scalar(out=bits[0:1, :], in0=bits_raw[:], scalar1=-1.0, scalar2=None, op0=ALU.add)
 
-        def do_BX(c4, eng):
-            dst = cbm[:, 512 * c4 : 512 * c4 + 512]
-            if eng == "V":
-                nc.vector.tensor_scalar(out=dst, in0=bank[("B", c4)][:], scalar1=-1.0, scalar2=None, op0=ALU.add)
-            else:
-                nc.scalar.activation(out=dst, in_=bank[("B", c4)][:], func=ACT.Copy, bias=-1.0, scale=1.0)
+        def do_BM(b):
+            bank[("B", b)] = ps_mm.tile([P, 1024], BF16, name="pb", tag="mm")
+            for h in range(2):
+                nc.tensor.matmul(
+                    out=bank[("B", b)][:, 512 * h : 512 * h + 512], lhsT=ones[:],
+                    rhs=bits[:, 1024 * b + 512 * h : 1024 * b + 512 * h + 512], start=True, stop=True,
+                )
+
+        def do_BX(b, eng):
+            copy_out(eng, cbm[:, 1024 * b : 1024 * b + 1024], bank[("B", b)][:])
 
         def do_TP(x, g, a2):
             words = rawt[x][:].bitcast(F32)
@@ -213,10 +217,19 @@ def tile_attention_pa_kernel(tc, query, context, query_bit, context_bit, W_in, b
                     bias=bias_f[:, 4 * g2 + n : 4 * g2 + n + 1], scale=1.0,
                 )
 
-        def do_RG(b, g2, eng):
-            grp[("g", b, g2)] = stage.tile([P, 2048], BF16, name="qg", tag="qg", bufs=4, align_bytes=64)
-            dst = grp[("g", b, g2)][:].rearrange("p (c i t) -> p c t i", i=4, t=4)
-            src = grp[("p", b, g2)][:].rearrange("p (t c i) -> p c t i", t=4, i=4)
+        def do_RG(b, g2, *rest):
+            eng = rest[-1]
+            if ("g", b, g2) not in grp:
+                grp[("g", b, g2)] = stage.tile([P, 2048], BF16, name="qg", tag="qg", bufs=4, align_bytes=64)
+            if len(rest) == 1:
+                dst = grp[("g", b, g2)][:].rearrange("p (c i t) -> p c t i", i=4, t=4)
+                src = grp[("p", b, g2)][:].rearrange("p (t c i) -> p c t i", t=4, i=4)
+            else:
+                h = rest[0]
+                dst = grp[("g", b, g2)][:, 1024 * h : 1024 * h + 1024].rearrange("p (c i t) -> p c t i", i=4, t=4)
+                src = grp[("p", b, g2)][:].rearrange("p (t w) -> p t w", t=4)[:, :, 256 * h : 256 * h + 256].rearrange(
+                    "p t (c i) -> p c t i", i=4
+                )
             if eng == "V":
                 nc.vector.tensor_copy(out=dst, in_=src)
             else:
@@ -225,8 +238,10 @@ def tile_attention_pa_kernel(tc, query, context, query_bit, context_bit, W_in, b
         def do_QZ2(b, g2, n=None):
             if n is None:
                 quantise(("z%d" % b, g2, 0), 512, grp[("g", b, g2)][:])
-            else:
+            elif ROUTE[(b, g2)] == "V":
                 quantise(("z%d" % b, g2, n), 128, grp[("g", b, g2)][:, 512 * n : 512 * n + 512])
+            else:
+                quantise(("z%d" % b, g2, n), 256, grp[("g", b, g2)][:, 1024 * n : 1024 * n + 1024])
 
         def do_M2(b, n, jh):
             acc = ps_mm.tile([P, 512], F32, name="acc2", tag="mm")
@@ -234,6 +249,8 @@ def tile_attention_pa_kernel(tc, query, context, query_bit, context_bit, W_in, b
             for g2 in range(2):
                 if ROUTE[(b, g2)] == "V":
                     wkey, wcols = ("z%d" % b, g2, n), slice(0, 128)
+                elif RG_HALVES:
+                    wkey, wcols = ("z%d" % b, g2, n // 2), slice(128 * (n % 2), 128 * (n % 2) + 128)
                 else:
                     wkey, wcols = ("z%d" % b, g2, 0), slice(128 * n, 128 * n + 128)
                 mx(acc[:], wkey, wcols, ("c%d%d" % (b, jh), g2, 0), slice(0, 512), g2 == 0, g2 == 1)
@@ -242,10 +259,10 @@ def tile_attention_pa_kernel(tc, query, context, query_bit, context_bit, W_in, b
             if (b, n) not in sm:
                 sm[(b, n)] = soft.tile([P, 1024], F32, name="sm", tag="sm")
             nc.vector.scalar_tensor_tensor(
-                out=sm[(b, n)][:, 512 * jh : 512 * jh + 512],
-                in0=cbm[:, 1024 * b + 512 * jh : 1024 * b + 512 * jh + 512],
+                out=sm[(b, n)][:, 512 * jh : 512 * jh + 512].rearrange("p (r c) -> p r c", c=4),
+                in0=cbm[:, 1024 * b + 512 * jh : 1024 * b + 512 * jh + 512].rearrange("p (r c) -> p r c", c=4),
                 scalar=s10k[:, 4 * b + n : 4 * b + n + 1],
-                in1=bank[("2", b, n, jh)][:],
+                in1=bank[("2", b, n, jh)][:].rearrange("p (c r) -> p r c", c=4),
                 op0=ALU.mult,
                 op1=ALU.add,
             )
@@ -265,23 +282,26 @@ def tile_attention_pa_kernel(tc, query, context, query_bit, context_bit, W_in, b
             tiny[("r", b, n)] = small.tile([P, 1], F32, name="rs", tag="rs")
             nc.vector.reciprocal(tiny[("r", b, n)][:], tiny[("s", b, n)][:])
 
-        def do_G(b, n, eng):
-            s = sm[(b, n)]
+        def do_G(b, n, *rest):
+            eng = rest[-1]
+            cols = slice(0, 1024) if len(rest) == 1 else slice(512 * rest[0], 512 * rest[0] + 512)
+            s = sm[(b, n)][:, cols]
             rs = tiny[("r", b, n)]
             if eng == "S":
-                nc.scalar.activation(out=s[:], in_=s[:], func=ACT.Copy, scale=rs[:])
+                nc.scalar.activation(out=s, in_=s, func=ACT.Copy, scale=rs[:])
             elif eng == "V":
-                nc.vector.tensor_scalar(out=s[:], in0=s[:], scalar1=rs[:], scalar2=None, op0=ALU.mult)
+                nc.vector.tensor_scalar(out=s, in0=s, scalar1=rs[:], scalar2=None, op0=ALU.mult)
             else:
-                nc.gpsimd.tensor_scalar(out=s[:], in0=s[:], scalar1=rs[:], scalar2=0.0, op0=ALU.mult, op1=ALU.add)
+                nc.gpsimd.tensor_scalar(out=s, in0=s, scalar1=rs[:], scalar2=0.0, op0=ALU.mult, op1=ALU.add)
 
-        def do_ST(b, n):
-            nc.sync.dma_start(out=out[b].rearrange("(p n) j -> p n j", n=4)[:, n, :], in_=sm[(b, n)][:])
+        def do_ST(b, n, *rest):
+            cols = slice(0, 1024) if len(rest) == 0 else slice(512 * rest[0], 512 * rest[0] + 512)
+            nc.sync.dma_start(out=out[b].rearrange("(p n) j -> p n j", n=4)[:, n, cols], in_=sm[(b, n)][:, cols])
 
         table = {
             "L": do_L, "LB": do_LB, "BM": do_BM, "BX": do_BX, "TP": do_TP, "EX": do_EX, "QZ": do_QZ, "M1": do_M1,
             "X1": do_X1, "RG": do_RG, "QZ2": do_QZ2, "M2": do_M2, "D": do_D, "E": do_E, "F": do_F, "R": do_R,
-            "G": do_G, "ST": do_ST, "CB": do_CB, "CS": do_CS,
+            "G": do_G, "ST": do_ST, "CB": do_CB, "CS": do_CS, "CM": do_CM,
         }
         for step in ORDER:
             table[step[0]](*step[1:])

@@ -15,49 +15,49 @@ AX = mybir.AxisListType
 P = 128
 FLOPS = 2 * 1024 * 1024 * 1024 + 2 * 2 * 512 * 1024 * 1024
 
-ROUTE = {(0, 0): "S", (0, 1): "S", (1, 0): "S", (1, 1): "S"}
+ROUTE = {(0, 0): "V", (0, 1): "V", (1, 0): "S", (1, 1): "S"}
 
 RG_HALVES = True
 
 ORDER = [
     ("L", "q0", 0), ("LB",), ("L", "q0", 1), ("L", "W0", 0), ("L", "W0", 1), ("L", "W1", 0),
     ("L", "W1", 1), ("L", "c00", 0), ("L", "c00", 1), ("L", "c01", 0), ("L", "c01", 1), ("L", "q1", 0),
-    ("L", "q1", 1), ("L", "c10", 0), ("L", "c10", 1), ("L", "c11", 0), ("L", "c11", 1), ("TP", "q0", 1, 0),
-    ("CM",), ("TP", "q0", 0, 0), ("EX", "q0", 1, 0, "S"), ("BM", 1), ("EX", "q0", 0, 0, "V"), ("TP", "q0", 1, 1),
-    ("BX", 1, "S"), ("TP", "q0", 0, 1), ("EX", "q0", 1, 1, "V"), ("EX", "q0", 0, 1, "S"), ("TP", "W0", 0, 0), ("QZ", "q0", 1),
-    ("TP", "W0", 1, 0), ("EX", "W0", 0, 0, "S"), ("QZ", "q0", 0), ("EX", "W0", 1, 0, "S"), ("TP", "W0", 0, 1), ("TP", "W0", 1, 1),
-    ("EX", "W0", 0, 1, "S"), ("BM", 0), ("EX", "W0", 1, 1, "S"), ("QZ", "W0", 0), ("TP", "W1", 1, 0), ("TP", "W1", 0, 0),
-    ("BX", 0, "S"), ("QZ", "W0", 1), ("TP", "W1", 0, 1), ("EX", "W1", 0, 0, "V"), ("TP", "W1", 1, 1), ("EX", "W1", 0, 1, "V"),
-    ("CB",), ("M1", 0, 0, 2), ("EX", "W1", 1, 0, "V"), ("M1", 0, 0, 3), ("X1", 0, 0, 2), ("M1", 0, 0, 0),
-    ("QZ", "W1", 0), ("X1", 0, 0, 3), ("M1", 0, 0, 1), ("EX", "W1", 1, 1, "V"), ("X1", 0, 0, 0), ("TP", "c00", 0, 0),
-    ("QZ", "W1", 1), ("X1", 0, 0, 1), ("TP", "c00", 0, 1), ("TP", "c01", 1, 0), ("EX", "c00", 0, 0, "V"), ("EX", "c00", 0, 1, "S"),
-    ("TP", "c01", 0, 0), ("RG", 0, 0, 0, "P"), ("EX", "c01", 1, 0, "V"), ("M1", 0, 1, 0), ("EX", "c01", 0, 0, "S"), ("QZ", "c00", 0),
-    ("M1", 0, 1, 3), ("X1", 0, 1, 0), ("RG", 0, 0, 1, "P"), ("M1", 0, 1, 1), ("QZ2", 0, 0, 0), ("X1", 0, 1, 3),
-    ("TP", "q1", 1, 0), ("X1", 0, 1, 1), ("TP", "c01", 1, 1), ("EX", "q1", 1, 0, "V"), ("TP", "q1", 0, 0), ("EX", "c01", 1, 1, "S"),
-    ("TP", "c01", 0, 1), ("QZ2", 0, 0, 1), ("M1", 0, 1, 2), ("EX", "q1", 0, 0, "S"), ("EX", "c01", 0, 1, "V"), ("TP", "c00", 1, 1),
-    ("QZ", "c01", 0), ("X1", 0, 1, 2), ("TP", "c10", 1, 0), ("QZ", "c01", 1), ("TP", "c00", 1, 0), ("EX", "c00", 1, 1, "S"),
-    ("RG", 0, 1, 0, "P"), ("TP", "q1", 1, 1), ("EX", "c00", 1, 0, "V"), ("EX", "c10", 1, 0, "S"), ("TP", "q1", 0, 1), ("QZ", "c00", 1),
-    ("EX", "q1", 1, 1, "S"), ("TP", "c10", 1, 1), ("RG", 0, 1, 1, "P"), ("EX", "q1", 0, 1, "S"), ("QZ2", 0, 1, 0), ("TP", "c11", 1, 0),
-    ("QZ", "q1", 1), ("TP", "c11", 0, 0), ("EX", "c10", 1, 1, "S"), ("CS",), ("M2", 0, 1, 0), ("QZ", "q1", 0),
-    ("EX", "c11", 1, 0, "S"), ("M2", 0, 1, 1), ("QZ2", 0, 1, 1), ("EX", "c11", 0, 0, "S"), ("D", 0, 1, 0), ("M1", 1, 0, 1),
-    ("D", 0, 1, 1), ("TP", "c11", 1, 1), ("TP", "c11", 0, 1), ("E", 0, 1), ("EX", "c11", 1, 1, "S"), ("M2", 0, 2, 0),
-    ("X1", 1, 0, 1), ("M1", 1, 0, 0), ("D", 0, 2, 0), ("EX", "c11", 0, 1, "S"), ("M1", 1, 1, 3), ("QZ", "c10", 1),
-    ("X1", 1, 0, 0), ("M2", 0, 2, 1), ("QZ", "c11", 0), ("X1", 1, 1, 3), ("M1", 1, 0, 2), ("D", 0, 2, 1),
-    ("M1", 1, 0, 3), ("X1", 1, 0, 2), ("QZ", "c11", 1), ("M1", 1, 1, 0), ("X1", 1, 0, 3), ("E", 0, 2),
-    ("M2", 0, 3, 1), ("X1", 1, 1, 0), ("RG", 1, 0, 0, "P"), ("M2", 0, 0, 1), ("F", 0, 1), ("M2", 0, 0, 0),
-    ("D", 0, 3, 1), ("M1", 1, 1, 1), ("D", 0, 0, 1), ("RG", 1, 0, 1, "P"), ("M1", 1, 1, 2), ("D", 0, 0, 0),
-    ("X1", 1, 1, 1), ("TP", "c10", 0, 0), ("QZ2", 1, 0, 0), ("X1", 1, 1, 2), ("TP", "c10", 0, 1), ("E", 0, 0),
-    ("EX", "c10", 0, 0, "S"), ("M2", 0, 3, 0), ("RG", 1, 1, 0, "P"), ("EX", "c10", 0, 1, "S"), ("D", 0, 3, 0), ("F", 0, 2),
-    ("E", 0, 3), ("RG", 1, 1, 1, "P"), ("QZ2", 1, 1, 0), ("F", 0, 3), ("R", 0, 2), ("R", 0, 1),
-    ("QZ", "c10", 0), ("G", 0, 1, "P"), ("M2", 1, 0, 1), ("QZ2", 1, 0, 1), ("M2", 1, 1, 1), ("F", 0, 0),
-    ("QZ2", 1, 1, 1), ("D", 1, 0, 1), ("G", 0, 2, "P"), ("M2", 1, 0, 0), ("ST", 0, 1), ("D", 1, 1, 1),
-    ("M2", 1, 1, 0), ("M2", 1, 3, 1), ("R", 0, 3), ("D", 1, 0, 0), ("G", 0, 3, "P"), ("M2", 1, 2, 0),
-    ("D", 1, 1, 0), ("M2", 1, 3, 0), ("R", 0, 0), ("E", 1, 0), ("G", 0, 0, "P"), ("M2", 1, 2, 1),
-    ("D", 1, 3, 0), ("F", 1, 0), ("ST", 0, 0), ("ST", 0, 2), ("E", 1, 1), ("R", 1, 0),
-    ("D", 1, 2, 1), ("F", 1, 1), ("G", 1, 0, "P"), ("D", 1, 2, 0), ("E", 1, 2), ("ST", 1, 0),
-    ("ST", 0, 3), ("R", 1, 1), ("D", 1, 3, 1), ("F", 1, 2), ("G", 1, 1, "P"), ("E", 1, 3),
-    ("ST", 1, 1), ("R", 1, 2), ("G", 1, 2, "V"), ("F", 1, 3), ("ST", 1, 2), ("R", 1, 3),
-    ("G", 1, 3, 1, "V"), ("G", 1, 3, 0, "V"), ("ST", 1, 3, 1), ("ST", 1, 3, 0),
+    ("L", "q1", 1), ("L", "c10", 0), ("L", "c10", 1), ("L", "c11", 0), ("L", "c11", 1), ("TP", "q0", 0, 0),
+    ("CM",), ("TP", "q0", 1, 0), ("BM", 0), ("EX", "q0", 1, 0, "S"), ("EX", "q0", 0, 0, "S"), ("TP", "q0", 0, 1),
+    ("TP", "q0", 1, 1), ("EX", "q0", 0, 1, "V"), ("EX", "q0", 1, 1, "S"), ("TP", "W0", 1, 0), ("TP", "W0", 0, 0), ("QZ", "q0", 1),
+    ("EX", "W0", 0, 0, "S"), ("TP", "W0", 1, 1), ("QZ", "q0", 0), ("EX", "W0", 1, 0, "S"), ("TP", "W0", 0, 1), ("EX", "W0", 1, 1, "V"),
+    ("BM", 1), ("EX", "W0", 0, 1, "S"), ("QZ", "W0", 1), ("TP", "W1", 0, 0), ("BX", 1, "S"), ("TP", "W1", 1, 0),
+    ("QZ", "W0", 0), ("TP", "W1", 1, 1), ("EX", "W1", 0, 0, "V"), ("TP", "W1", 0, 1), ("EX", "W1", 1, 1, "S"), ("EX", "W1", 1, 0, "V"),
+    ("CB",), ("M1", 0, 0, 1), ("EX", "W1", 0, 1, "S"), ("QZ", "W1", 1), ("M1", 0, 0, 0), ("BX", 0, "S"),
+    ("QZ", "W1", 0), ("TP", "c00", 1, 0), ("TP", "c00", 0, 0), ("X1", 0, 0, 1), ("EX", "c00", 1, 0, "S"), ("TP", "c00", 1, 1),
+    ("TP", "c00", 0, 1), ("X1", 0, 0, 0), ("EX", "c00", 1, 1, "S"), ("M1", 0, 1, 1), ("EX", "c00", 0, 0, "V"), ("EX", "c00", 0, 1, "S"),
+    ("M1", 0, 0, 3), ("X1", 0, 1, 1), ("M1", 0, 1, 0), ("QZ", "c00", 1), ("M1", 0, 0, 2), ("QZ2", 0, 0, 0),
+    ("QZ2", 0, 1, 1), ("X1", 0, 1, 0), ("TP", "c01", 1, 0), ("TP", "q1", 1, 0), ("X1", 0, 0, 2), ("EX", "c01", 1, 0, "S"),
+    ("TP", "q1", 0, 0), ("QZ2", 0, 0, 1), ("M1", 0, 1, 2), ("EX", "q1", 1, 0, "S"), ("X1", 0, 0, 3), ("EX", "q1", 0, 0, "S"),
+    ("TP", "q1", 1, 1), ("X1", 0, 1, 2), ("TP", "q1", 0, 1), ("EX", "q1", 1, 1, "S"), ("TP", "c01", 0, 0), ("QZ2", 0, 0, 2),
+    ("QZ2", 0, 1, 2), ("TP", "c01", 0, 1), ("QZ", "c00", 0), ("EX", "q1", 0, 1, "S"), ("TP", "c01", 1, 1), ("QZ2", 0, 1, 0),
+    ("EX", "c01", 0, 1, "S"), ("M1", 0, 1, 3), ("QZ", "q1", 1), ("EX", "c01", 0, 0, "S"), ("CS",), ("M2", 0, 0, 0),
+    ("QZ", "q1", 0), ("EX", "c01", 1, 1, "S"), ("TP", "c10", 1, 1), ("D", 0, 0, 0), ("TP", "c11", 1, 0), ("EX", "c10", 1, 1, "S"),
+    ("TP", "c10", 1, 0), ("QZ", "c01", 1), ("M1", 1, 0, 3), ("EX", "c10", 1, 0, "S"), ("X1", 0, 1, 3), ("M2", 0, 2, 0),
+    ("EX", "c11", 1, 0, "S"), ("QZ", "c01", 0), ("M1", 1, 0, 2), ("X1", 1, 0, 3), ("D", 0, 2, 0), ("M2", 0, 1, 0),
+    ("X1", 1, 0, 2), ("QZ2", 0, 0, 3), ("M1", 1, 0, 0), ("QZ2", 0, 1, 3), ("D", 0, 1, 0), ("M2", 0, 1, 1),
+    ("X1", 1, 0, 0), ("QZ", "c10", 1), ("M1", 1, 0, 1), ("D", 0, 1, 1), ("M2", 0, 2, 1), ("X1", 1, 0, 1),
+    ("E", 0, 1), ("TP", "c11", 0, 0), ("RG", 1, 0, 1, "P"), ("TP", "c11", 0, 1), ("EX", "c11", 0, 0, "S"), ("TP", "c11", 1, 1),
+    ("D", 0, 2, 1), ("M1", 1, 1, 0), ("EX", "c11", 0, 1, "S"), ("E", 0, 2), ("M2", 0, 0, 1), ("EX", "c11", 1, 1, "S"),
+    ("RG", 1, 0, 0, "P"), ("M1", 1, 1, 2), ("X1", 1, 1, 0), ("D", 0, 0, 1), ("M1", 1, 1, 1), ("X1", 1, 1, 2),
+    ("QZ", "c11", 1), ("M1", 1, 1, 3), ("X1", 1, 1, 1), ("M2", 0, 3, 1), ("QZ2", 1, 0, 1), ("X1", 1, 1, 3),
+    ("QZ", "c11", 0), ("M2", 0, 3, 0), ("F", 0, 2), ("D", 0, 3, 1), ("RG", 1, 1, 0, "P"), ("TP", "c10", 0, 1),
+    ("TP", "c10", 0, 0), ("D", 0, 3, 0), ("EX", "c10", 0, 1, "S"), ("E", 0, 0), ("RG", 1, 1, 1, "P"), ("F", 0, 1),
+    ("E", 0, 3), ("EX", "c10", 0, 0, "S"), ("QZ2", 1, 1, 1), ("F", 0, 0), ("QZ2", 1, 0, 0), ("R", 0, 2),
+    ("R", 0, 1), ("QZ2", 1, 1, 0), ("M2", 1, 3, 1), ("QZ", "c10", 0), ("F", 0, 3), ("M2", 1, 0, 1),
+    ("D", 1, 3, 1), ("G", 0, 1, "P"), ("M2", 1, 0, 0), ("R", 0, 0), ("D", 1, 0, 1), ("G", 0, 0, "S"),
+    ("M2", 1, 1, 1), ("G", 0, 2, "P"), ("ST", 0, 1), ("R", 0, 3), ("D", 1, 0, 0), ("M2", 1, 2, 1),
+    ("G", 0, 3, "S"), ("E", 1, 0), ("M2", 1, 2, 0), ("ST", 0, 0), ("M2", 1, 3, 0), ("D", 1, 1, 1),
+    ("ST", 0, 3), ("F", 1, 0), ("ST", 0, 2), ("D", 1, 3, 0), ("M2", 1, 1, 0), ("E", 1, 3),
+    ("D", 1, 1, 0), ("F", 1, 3), ("R", 1, 0), ("E", 1, 1), ("G", 1, 0, "S"), ("R", 1, 3),
+    ("D", 1, 2, 1), ("G", 1, 3, 1, "P"), ("G", 1, 3, 0, "S"), ("D", 1, 2, 0), ("ST", 1, 0), ("ST", 1, 3, 1),
+    ("F", 1, 1), ("E", 1, 2), ("ST", 1, 3, 0), ("F", 1, 2), ("R", 1, 1), ("G", 1, 1, "V"),
+    ("ST", 1, 1), ("R", 1, 2), ("G", 1, 2, "V"), ("ST", 1, 2),
 ]
 
 
@@ -74,6 +74,9 @@ def tile_attention_pa_kernel(tc, query, context, query_bit, context_bit, W_in, b
         ps_mm = ctx.enter_context(tc.psum_pool(name="ps_mm", bufs=4))
         ctx.enter_context(tc.manual_schedule())
 
+        warm = const.tile([P, 2], F32, name="warm")
+        nc.vector.memset(warm[:], 0.0)
+        nc.scalar.activation(out=warm[:, 1:2], in_=warm[:, 0:1], func=ACT.Exp)
         bits = const.tile([P, 2048], BF16, name="bits")
         nc.vector.memset(bits[:], 0.0)
         bits_raw = const.tile([1, 2048], BF16, name="bits_raw")

@@ -13,298 +13,328 @@ ACT = mybir.ActivationFunctionType
 AX = mybir.AxisListType
 
 P = 128
+BANK = 512
+FEATURES = 1024
+CONTEXT_ROWS = 1024
+MASKED = 10000.0
+
+GROUPS = ["q0", "w0", "w1", "c00", "c01", "q1", "c10", "c11"]
+
 FLOPS = 2 * 1024 * 1024 * 1024 + 2 * 2 * 512 * 1024 * 1024
-
-ROUTE = {(0, 0): "V", (0, 1): "V", (1, 0): "S", (1, 1): "S"}
-
-RG_HALVES = True
-
-ORDER = [
-    ("L", "q0", 0), ("LB",), ("L", "q0", 1), ("L", "W0", 0), ("L", "W0", 1), ("L", "W1", 0),
-    ("L", "W1", 1), ("L", "c00", 0), ("L", "c00", 1), ("L", "c01", 0), ("L", "c01", 1), ("L", "q1", 0),
-    ("L", "q1", 1), ("L", "c10", 0), ("L", "c10", 1), ("L", "c11", 0), ("L", "c11", 1), ("TP", "q0", 0, 0),
-    ("CM",), ("TP", "q0", 1, 0), ("BM", 0), ("EX", "q0", 1, 0, "S"), ("EX", "q0", 0, 0, "S"), ("TP", "q0", 0, 1),
-    ("TP", "q0", 1, 1), ("EX", "q0", 0, 1, "V"), ("EX", "q0", 1, 1, "S"), ("TP", "W0", 1, 0), ("TP", "W0", 0, 0), ("QZ", "q0", 1),
-    ("EX", "W0", 0, 0, "S"), ("TP", "W0", 1, 1), ("QZ", "q0", 0), ("EX", "W0", 1, 0, "S"), ("TP", "W0", 0, 1), ("EX", "W0", 1, 1, "V"),
-    ("BM", 1), ("EX", "W0", 0, 1, "S"), ("QZ", "W0", 1), ("TP", "W1", 0, 0), ("BX", 1, "S"), ("TP", "W1", 1, 0),
-    ("QZ", "W0", 0), ("TP", "W1", 1, 1), ("EX", "W1", 0, 0, "V"), ("TP", "W1", 0, 1), ("EX", "W1", 1, 1, "S"), ("EX", "W1", 1, 0, "V"),
-    ("CB",), ("M1", 0, 0, 1), ("EX", "W1", 0, 1, "S"), ("QZ", "W1", 1), ("M1", 0, 0, 0), ("BX", 0, "S"),
-    ("QZ", "W1", 0), ("TP", "c00", 1, 0), ("TP", "c00", 0, 0), ("X1", 0, 0, 1), ("EX", "c00", 1, 0, "S"), ("TP", "c00", 1, 1),
-    ("TP", "c00", 0, 1), ("X1", 0, 0, 0), ("EX", "c00", 1, 1, "S"), ("M1", 0, 1, 1), ("EX", "c00", 0, 0, "V"), ("EX", "c00", 0, 1, "S"),
-    ("M1", 0, 0, 3), ("X1", 0, 1, 1), ("M1", 0, 1, 0), ("QZ", "c00", 1), ("M1", 0, 0, 2), ("QZ2", 0, 0, 0),
-    ("QZ2", 0, 1, 1), ("X1", 0, 1, 0), ("TP", "c01", 1, 0), ("TP", "q1", 1, 0), ("X1", 0, 0, 2), ("EX", "c01", 1, 0, "S"),
-    ("TP", "q1", 0, 0), ("QZ2", 0, 0, 1), ("M1", 0, 1, 2), ("EX", "q1", 1, 0, "S"), ("X1", 0, 0, 3), ("EX", "q1", 0, 0, "S"),
-    ("TP", "q1", 1, 1), ("X1", 0, 1, 2), ("TP", "q1", 0, 1), ("EX", "q1", 1, 1, "S"), ("TP", "c01", 0, 0), ("QZ2", 0, 0, 2),
-    ("QZ2", 0, 1, 2), ("TP", "c01", 0, 1), ("QZ", "c00", 0), ("EX", "q1", 0, 1, "S"), ("TP", "c01", 1, 1), ("QZ2", 0, 1, 0),
-    ("EX", "c01", 0, 1, "S"), ("M1", 0, 1, 3), ("QZ", "q1", 1), ("EX", "c01", 0, 0, "S"), ("CS",), ("M2", 0, 0, 0),
-    ("QZ", "q1", 0), ("EX", "c01", 1, 1, "S"), ("TP", "c10", 1, 1), ("D", 0, 0, 0), ("TP", "c11", 1, 0), ("EX", "c10", 1, 1, "S"),
-    ("TP", "c10", 1, 0), ("QZ", "c01", 1), ("M1", 1, 0, 3), ("EX", "c10", 1, 0, "S"), ("X1", 0, 1, 3), ("M2", 0, 2, 0),
-    ("EX", "c11", 1, 0, "S"), ("QZ", "c01", 0), ("M1", 1, 0, 2), ("X1", 1, 0, 3), ("D", 0, 2, 0), ("M2", 0, 1, 0),
-    ("X1", 1, 0, 2), ("QZ2", 0, 0, 3), ("M1", 1, 0, 0), ("QZ2", 0, 1, 3), ("D", 0, 1, 0), ("M2", 0, 1, 1),
-    ("X1", 1, 0, 0), ("QZ", "c10", 1), ("M1", 1, 0, 1), ("D", 0, 1, 1), ("M2", 0, 2, 1), ("X1", 1, 0, 1),
-    ("E", 0, 1), ("TP", "c11", 0, 0), ("RG", 1, 0, 1, "P"), ("TP", "c11", 0, 1), ("EX", "c11", 0, 0, "S"), ("TP", "c11", 1, 1),
-    ("D", 0, 2, 1), ("M1", 1, 1, 0), ("EX", "c11", 0, 1, "S"), ("E", 0, 2), ("M2", 0, 0, 1), ("EX", "c11", 1, 1, "S"),
-    ("RG", 1, 0, 0, "P"), ("M1", 1, 1, 2), ("X1", 1, 1, 0), ("D", 0, 0, 1), ("M1", 1, 1, 1), ("X1", 1, 1, 2),
-    ("QZ", "c11", 1), ("M1", 1, 1, 3), ("X1", 1, 1, 1), ("M2", 0, 3, 1), ("QZ2", 1, 0, 1), ("X1", 1, 1, 3),
-    ("QZ", "c11", 0), ("M2", 0, 3, 0), ("F", 0, 2), ("D", 0, 3, 1), ("RG", 1, 1, 0, "P"), ("TP", "c10", 0, 1),
-    ("TP", "c10", 0, 0), ("D", 0, 3, 0), ("EX", "c10", 0, 1, "S"), ("E", 0, 0), ("RG", 1, 1, 1, "P"), ("F", 0, 1),
-    ("E", 0, 3), ("EX", "c10", 0, 0, "S"), ("QZ2", 1, 1, 1), ("F", 0, 0), ("QZ2", 1, 0, 0), ("R", 0, 2),
-    ("R", 0, 1), ("QZ2", 1, 1, 0), ("M2", 1, 3, 1), ("QZ", "c10", 0), ("F", 0, 3), ("M2", 1, 0, 1),
-    ("D", 1, 3, 1), ("G", 0, 1, "P"), ("M2", 1, 0, 0), ("R", 0, 0), ("D", 1, 0, 1), ("G", 0, 0, "S"),
-    ("M2", 1, 1, 1), ("G", 0, 2, "P"), ("ST", 0, 1), ("R", 0, 3), ("D", 1, 0, 0), ("M2", 1, 2, 1),
-    ("G", 0, 3, "S"), ("E", 1, 0), ("M2", 1, 2, 0), ("ST", 0, 0), ("M2", 1, 3, 0), ("D", 1, 1, 1),
-    ("ST", 0, 3), ("F", 1, 0), ("ST", 0, 2), ("D", 1, 3, 0), ("M2", 1, 1, 0), ("E", 1, 3),
-    ("D", 1, 1, 0), ("F", 1, 3), ("R", 1, 0), ("E", 1, 1), ("G", 1, 0, "S"), ("R", 1, 3),
-    ("D", 1, 2, 1), ("G", 1, 3, 1, "P"), ("G", 1, 3, 0, "S"), ("D", 1, 2, 0), ("ST", 1, 0), ("ST", 1, 3, 1),
-    ("F", 1, 1), ("E", 1, 2), ("ST", 1, 3, 0), ("F", 1, 2), ("R", 1, 1), ("G", 1, 1, "V"),
-    ("ST", 1, 1), ("R", 1, 2), ("G", 1, 2, "V"), ("ST", 1, 2),
-]
 
 
 def tile_attention_pa_kernel(tc, query, context, query_bit, context_bit, W_in, b_in, out):
     nc = tc.nc
     with ExitStack() as ctx:
         const = ctx.enter_context(tc.tile_pool(name="const", bufs=1))
-        raw = ctx.enter_context(tc.tile_pool(name="raw", bufs=1))
-        keep = ctx.enter_context(tc.tile_pool(name="keep", bufs=1))
-        stage = ctx.enter_context(tc.tile_pool(name="stage", bufs=8))
+        loaded = ctx.enter_context(tc.tile_pool(name="loaded", bufs=1))
+        packed = ctx.enter_context(tc.tile_pool(name="packed", bufs=1))
+        staging = ctx.enter_context(tc.tile_pool(name="staging", bufs=8))
         soft = ctx.enter_context(tc.tile_pool(name="soft", bufs=8))
-        small = ctx.enter_context(tc.tile_pool(name="small", bufs=8))
-        ps_tp = ctx.enter_context(tc.psum_pool(name="ps_tp", bufs=4))
-        ps_mm = ctx.enter_context(tc.psum_pool(name="ps_mm", bufs=4))
+        stats = ctx.enter_context(tc.tile_pool(name="stats", bufs=8))
+        turned = ctx.enter_context(tc.psum_pool(name="turned", bufs=4))
+        sums = ctx.enter_context(tc.psum_pool(name="sums", bufs=4))
         ctx.enter_context(tc.manual_schedule())
 
         warm = const.tile([P, 2], F32, name="warm")
         nc.vector.memset(warm[:], 0.0)
         nc.scalar.activation(out=warm[:, 1:2], in_=warm[:, 0:1], func=ACT.Exp)
-        bits = const.tile([P, 2048], BF16, name="bits")
-        nc.vector.memset(bits[:], 0.0)
-        bits_raw = const.tile([1, 2048], BF16, name="bits_raw")
+
+        mask_rows = const.tile([P, 2 * CONTEXT_ROWS], BF16, name="mask_rows")
+        nc.vector.memset(mask_rows[:], 0.0)
         ones = const.tile([P, P], BF16, name="ones")
         nc.vector.memset(ones[:], 1.0)
-        qb_raw = const.tile([P, 8], BF16, name="qb_raw")
-        b_raw = const.tile([P, 8], BF16, name="b_raw")
-        s10k = const.tile([P, 8], F32, name="s10k")
-        bias_f = const.tile([P, 8], F32, name="bias_f")
-        cbm = const.tile([P, 2048], BF16, name="cbm")
-        ident = const.tile([P, P], F32, name="ident")
-        make_identity(nc, ident[:])
+        identity = const.tile([P, P], F32, name="identity")
+        make_identity(nc, identity[:])
+        bits_row = const.tile([1, 2 * CONTEXT_ROWS], BF16, name="bits_row")
+        mask = const.tile([P, 2 * CONTEXT_ROWS], BF16, name="mask")
+        bias_bf16 = const.tile([P, 8], BF16, name="bias_bf16")
+        bias = const.tile([P, 8], F32, name="bias")
+        query_bits = const.tile([P, 8], BF16, name="query_bits")
+        penalty = const.tile([P, 8], F32, name="penalty")
 
-        rawt = {}
+        raw = {}
+        grouped = {}
         codes = {}
         scales = {}
-        bank = {}
-        grp = {}
-        sm = {}
-        tiny = {}
+        mask_bank = {}
+        q_planes = {}
+        q_grouped = {}
+        q_words = {}
+        score = {}
+        negative_max = {}
+        row_sum = {}
+        inverse_sum = {}
 
-        def copy_out(eng, dst, src):
-            if eng == "V":
-                nc.vector.tensor_copy(out=dst, in_=src)
+        def load(group, half):
+            if half == 0:
+                raw[group] = loaded.tile([P, 4 * FEATURES], BF16, name="raw_" + group)
+            if group[0] == "q":
+                rows = query[int(group[1])].rearrange("(p n) d -> p n d", n=4)[:, 2 * half : 2 * half + 2, :]
+            elif group[0] == "w":
+                first = 512 * int(group[1]) + 256 * half
+                rows = W_in[first : first + 256, :].rearrange("(p v) d -> p v d", v=2)
             else:
-                nc.scalar.copy(out=dst, in_=src)
+                first = 512 * int(group[2])
+                rows = context[int(group[1]), first : first + 512, :].rearrange("(p c) e -> p c e", c=4)
+                rows = rows[:, 2 * half : 2 * half + 2, :]
+            nc.sync.dma_start(
+                out=raw[group][:, 2 * FEATURES * half : 2 * FEATURES * (half + 1)].rearrange("p (n k) -> p n k", n=2),
+                in_=rows,
+            )
 
-        def quantise(key, width, grouped):
-            codes[key] = keep.tile([P, width], U32, name="c_%s_%d_%d" % key, align_bytes=64)
-            scales[key] = keep.tile([P, width], U8, name="s_%s_%d_%d" % key, align_bytes=64)
-            nc.vector.quantize_mx(out=codes[key][:].bitcast(FP8X4), scales=scales[key][:], in_=grouped)
+        def prepare(group, half, vector_helps):
+            words = raw[group][:].bitcast(F32)
+            for k_pass in range(2):
+                if half == 0:
+                    grouped[(group, k_pass)] = staging.tile([P, 4 * BANK], BF16, name="grouped", align_bytes=64)
+                bank = turned.tile([P, BANK], F32, name="bank")
+                for a in range(2):
+                    for u in range(2):
+                        first = 512 * (2 * half + a) + 256 * k_pass + 128 * u
+                        nc.tensor.transpose(
+                            bank[:, (2 * a + u) * P : (2 * a + u + 1) * P], words[:, first : first + P], identity[:]
+                        )
+                target = grouped[(group, k_pass)][:].bitcast(F32)[:, BANK * half : BANK * (half + 1)]
+                target = target.rearrange("p (a r u) -> p a r u", a=2, u=2)
+                source = bank[:].rearrange("p (a u r) -> p a r u", a=2, u=2)
+                if vector_helps and k_pass == 1:
+                    nc.vector.tensor_copy(out=target, in_=source)
+                else:
+                    nc.scalar.copy(out=target, in_=source)
 
-        def mx(acc, wkey, wcols, mkey, mcols, start, stop):
+        def quantise(operand, values):
+            width = values.shape[1] // 4
+            codes[operand] = packed.tile([P, width], U32, name="codes_%s_%d_%d" % operand, align_bytes=64)
+            scales[operand] = packed.tile([P, width], U8, name="scales_%s_%d_%d" % operand, align_bytes=64)
+            nc.vector.quantize_mx(out=codes[operand][:].bitcast(FP8X4), scales=scales[operand][:], in_=values)
+
+        def quantise_group(group):
+            for k_pass in range(2):
+                quantise((group, k_pass, 0), grouped[(group, k_pass)][:])
+
+        def multiply(acc, stationary, stationary_columns, moving, moving_columns, k_pass):
             nc.tensor.matmul_mx(
                 out=acc,
-                lhsT=codes[wkey][:, wcols].bitcast(FP8X4),
-                lhsT_scale=scales[wkey][:, wcols],
-                rhs=codes[mkey][:, mcols].bitcast(FP8X4),
-                rhs_scale=scales[mkey][:, mcols],
-                start=start,
-                stop=stop,
+                lhsT=codes[stationary][:, stationary_columns].bitcast(FP8X4),
+                lhsT_scale=scales[stationary][:, stationary_columns],
+                rhs=codes[moving][:, moving_columns].bitcast(FP8X4),
+                rhs_scale=scales[moving][:, moving_columns],
+                start=(k_pass == 0),
+                stop=(k_pass == 1),
             )
 
-        def do_L(x, a2):
-            if a2 == 0:
-                rawt[x] = raw.tile([P, 4096], BF16, name="raw_" + x)
-            if x[0] == "q":
-                src = query[int(x[1])].rearrange("(p n) d -> p n d", n=4)[:, 2 * a2 : 2 * a2 + 2, :]
-            elif x[0] == "W":
-                blk = 2 * int(x[1]) + a2
-                src = W_in[256 * blk : 256 * blk + 256, :].rearrange("(p e) d -> p e d", e=2)
-            else:
-                r0 = 512 * int(x[2])
-                src = context[int(x[1]), r0 : r0 + 512, :].rearrange("(p c) e -> p c e", c=4)[:, 2 * a2 : 2 * a2 + 2, :]
-            nc.sync.dma_start(out=rawt[x][:, 2048 * a2 : 2048 * a2 + 2048].rearrange("p (n d) -> p n d", n=2), in_=src)
-            if x == "W0" and a2 == 1:
-                nc.sync.dma_start(
-                    out=b_raw[:].rearrange("p (k e) -> p k e", k=4), in_=b_in.rearrange("(k p e) -> p k e", k=4, e=2)
-                )
-                nc.sync.dma_start(
-                    out=qb_raw[:].rearrange("p (b n) -> p b n", b=2), in_=query_bit.rearrange("b (p n) -> p b n", n=4)
-                )
+        def make_mask_row():
+            nc.vector.tensor_scalar(out=mask_rows[0:1, :], in0=bits_row[:], scalar1=-1.0, scalar2=None, op0=ALU.add)
 
-        def do_CB():
-            nc.vector.tensor_copy(out=bias_f[:], in_=b_raw[:])
-
-        def do_CS():
-            nc.vector.tensor_scalar(out=s10k[:], in0=qb_raw[:], scalar1=10000.0, scalar2=None, op0=ALU.mult)
-
-        def do_LB():
-            nc.sync.dma_start(out=bits_raw[:], in_=context_bit.rearrange("(o b) j -> o (b j)", o=1))
-
-        def do_CM():
-            nc.vector.tensor_scalar(out=bits[0:1, :], in0=bits_raw[:], scalar1=-1.0, scalar2=None, op0=ALU.add)
-
-        def do_BM(b):
-            bank[("B", b)] = ps_mm.tile([P, 1024], BF16, name="pb", tag="mm")
-            for h in range(2):
-                nc.tensor.matmul(
-                    out=bank[("B", b)][:, 512 * h : 512 * h + 512], lhsT=ones[:],
-                    rhs=bits[:, 1024 * b + 512 * h : 1024 * b + 512 * h + 512], start=True, stop=True,
-                )
-
-        def do_BX(b, eng):
-            copy_out(eng, cbm[:, 1024 * b : 1024 * b + 1024], bank[("B", b)][:])
-
-        def do_TP(x, g, a2):
-            words = rawt[x][:].bitcast(F32)
-            tp = ps_tp.tile([P, 512], F32, name="tp", tag="tp")
-            bank[("T", x, g, a2)] = tp
-            for a in range(2):
-                for u in range(2):
-                    col = (2 * a2 + a) * 512 + g * 256 + u * 128
-                    nc.tensor.transpose(
-                        tp[:, (2 * a + u) * 128 : (2 * a + u) * 128 + 128], words[:, col : col + 128], ident[:]
+        def spread_mask():
+            for b in range(2):
+                mask_bank[b] = sums.tile([P, CONTEXT_ROWS], BF16, name="mask_bank", tag="acc")
+                for h in range(2):
+                    first = CONTEXT_ROWS * b + BANK * h
+                    nc.tensor.matmul(
+                        out=mask_bank[b][:, BANK * h : BANK * (h + 1)],
+                        lhsT=ones[:],
+                        rhs=mask_rows[:, first : first + BANK],
+                        start=True,
+                        stop=True,
                     )
 
-        def do_EX(x, g, a2, eng):
-            if (x, g) not in grp:
-                grp[(x, g)] = stage.tile([P, 2048], BF16, name="grp", tag="grp", align_bytes=64)
-            dst = grp[(x, g)][:].bitcast(F32)[:, 512 * a2 : 512 * a2 + 512].rearrange("p (a r u) -> p a r u", a=2, u=2)
-            copy_out(eng, dst, bank[("T", x, g, a2)][:].rearrange("p (a u r) -> p a r u", a=2, u=2))
-
-        def do_QZ(x, g):
-            quantise((x, g, 0), 512, grp[(x, g)][:])
-
-        def do_M1(b, g2, n):
-            acc = ps_mm.tile([P, 512], F32, name="acc1", tag="mm")
-            bank[("1", b, g2, n)] = acc
-            wx = "W%d" % g2
-            qx = "q%d" % b
-            if ROUTE[(b, g2)] == "V":
-                for t in range(4):
-                    for g in range(2):
-                        mx(
-                            acc[:, 128 * t : 128 * t + 128],
-                            (wx, g, 0), slice(128 * t, 128 * t + 128),
-                            (qx, g, 0), slice(128 * n, 128 * n + 128),
-                            g == 0, g == 1,
-                        )
+        def copy_mask(b, on_vector):
+            target = mask[:, CONTEXT_ROWS * b : CONTEXT_ROWS * (b + 1)]
+            if on_vector:
+                nc.vector.tensor_copy(out=target, in_=mask_bank[b][:])
             else:
-                for g in range(2):
-                    mx(acc[:], (wx, g, 0), slice(128 * n, 128 * n + 128), (qx, g, 0), slice(0, 512), g == 0, g == 1)
+                nc.scalar.copy(out=target, in_=mask_bank[b][:])
 
-        def do_X1(b, g2, n):
-            acc = bank[("1", b, g2, n)]
-            if ROUTE[(b, g2)] == "V":
-                if ("g", b, g2) not in grp:
-                    grp[("g", b, g2)] = stage.tile([P, 2048], BF16, name="qg", tag="qg", bufs=4, align_bytes=64)
+        def project_on_vector(b, e_pass, half):
+            if half == 0:
+                q_grouped[(b, e_pass)] = staging.tile([P, 4 * BANK], BF16, name="q_grouped", bufs=4, align_bytes=64)
+            query_tiles = (2 * half, 2 * half + 1)
+            acc = {}
+            for n in query_tiles:
+                acc[n] = sums.tile([P, BANK], F32, name="acc")
+                for t in range(4):
+                    for d_pass in range(2):
+                        multiply(
+                            acc[n][:, P * t : P * (t + 1)],
+                            ("w%d" % e_pass, d_pass, 0), slice(P * t, P * (t + 1)),
+                            ("q%d" % b, d_pass, 0), slice(P * n, P * (n + 1)),
+                            d_pass,
+                        )
+            for n in query_tiles:
                 nc.vector.tensor_tensor(
-                    out=grp[("g", b, g2)][:, 512 * n : 512 * n + 512].rearrange("p (i t) -> p i t", t=4),
-                    in0=acc[:].rearrange("p (t i) -> p i t", t=4),
-                    in1=bias_f[:, 4 * g2 : 4 * g2 + 4].unsqueeze(1).to_broadcast([P, 128, 4]),
+                    out=q_grouped[(b, e_pass)][:, BANK * n : BANK * (n + 1)].rearrange("p (i t) -> p i t", t=4),
+                    in0=acc[n][:].rearrange("p (t i) -> p i t", t=4),
+                    in1=bias[:, 4 * e_pass : 4 * e_pass + 4].unsqueeze(1).to_broadcast([P, P, 4]),
                     op=ALU.add,
                 )
-            else:
-                if ("p", b, g2) not in grp:
-                    grp[("p", b, g2)] = stage.tile([P, 2048], BF16, name="qp", tag="qp", bufs=2)
+            for n in query_tiles:
+                quantise(("z%d" % b, e_pass, n), q_grouped[(b, e_pass)][:, BANK * n : BANK * (n + 1)])
+                q_words[(b, e_pass, n)] = (("z%d" % b, e_pass, n), slice(0, P))
+
+        def project_on_scalar(b, e_pass):
+            q_planes[(b, e_pass)] = staging.tile([P, 4 * BANK], BF16, name="q_planes", bufs=2)
+            q_grouped[(b, e_pass)] = staging.tile([P, 4 * BANK], BF16, name="q_grouped", bufs=4, align_bytes=64)
+            for t in range(4):
+                acc = sums.tile([P, BANK], F32, name="acc")
+                for d_pass in range(2):
+                    multiply(
+                        acc[:],
+                        ("w%d" % e_pass, d_pass, 0), slice(P * t, P * (t + 1)),
+                        ("q%d" % b, d_pass, 0), slice(0, BANK),
+                        d_pass,
+                    )
                 nc.scalar.activation(
-                    out=grp[("p", b, g2)][:, 512 * n : 512 * n + 512], in_=acc[:], func=ACT.Identity,
-                    bias=bias_f[:, 4 * g2 + n : 4 * g2 + n + 1], scale=1.0,
+                    out=q_planes[(b, e_pass)][:, BANK * t : BANK * (t + 1)],
+                    in_=acc[:],
+                    func=ACT.Identity,
+                    bias=bias[:, 4 * e_pass + t : 4 * e_pass + t + 1],
+                    scale=1.0,
+                )
+            planes = q_planes[(b, e_pass)][:].rearrange("p (t i) -> p t i", t=4)
+            for half in range(2):
+                target = q_grouped[(b, e_pass)][:, 2 * BANK * half : 2 * BANK * (half + 1)]
+                nc.gpsimd.tensor_scalar(
+                    out=target.rearrange("p (m f t) -> p m t f", f=4, t=4),
+                    in0=planes[:, :, 2 * P * half : 2 * P * (half + 1)].rearrange("p t (m f) -> p m t f", f=4),
+                    scalar1=1.0,
+                    scalar2=0.0,
+                    op0=ALU.mult,
+                    op1=ALU.add,
                 )
 
-        def do_RG(b, g2, *rest):
-            eng = rest[-1]
-            if ("g", b, g2) not in grp:
-                grp[("g", b, g2)] = stage.tile([P, 2048], BF16, name="qg", tag="qg", bufs=4, align_bytes=64)
-            if len(rest) == 1:
-                dst = grp[("g", b, g2)][:].rearrange("p (c i t) -> p c t i", i=4, t=4)
-                src = grp[("p", b, g2)][:].rearrange("p (t c i) -> p c t i", t=4, i=4)
-            else:
-                h = rest[0]
-                dst = grp[("g", b, g2)][:, 1024 * h : 1024 * h + 1024].rearrange("p (c i t) -> p c t i", i=4, t=4)
-                src = grp[("p", b, g2)][:].rearrange("p (t w) -> p t w", t=4)[:, :, 256 * h : 256 * h + 256].rearrange(
-                    "p t (c i) -> p c t i", i=4
+        def quantise_q(b, e_pass):
+            for half in range(2):
+                operand = ("z%d" % b, e_pass, half)
+                quantise(operand, q_grouped[(b, e_pass)][:, 2 * BANK * half : 2 * BANK * (half + 1)])
+                for a in range(2):
+                    q_words[(b, e_pass, 2 * half + a)] = (operand, slice(P * a, P * (a + 1)))
+
+        def scores(b, n):
+            score[(b, n)] = soft.tile([P, CONTEXT_ROWS], F32, name="score")
+            for h in range(2):
+                acc = sums.tile([P, BANK], F32, name="acc")
+                for e_pass in range(2):
+                    operand, columns = q_words[(b, e_pass, n)]
+                    multiply(acc[:], operand, columns, ("c%d%d" % (b, h), e_pass, 0), slice(0, BANK), e_pass)
+                first = CONTEXT_ROWS * b + BANK * h
+                nc.vector.scalar_tensor_tensor(
+                    out=score[(b, n)][:, BANK * h : BANK * (h + 1)].rearrange("p (r c) -> p r c", c=4),
+                    in0=mask[:, first : first + BANK].rearrange("p (r c) -> p r c", c=4),
+                    scalar=penalty[:, 4 * b + n : 4 * b + n + 1],
+                    in1=acc[:].rearrange("p (c r) -> p r c", c=4),
+                    op0=ALU.mult,
+                    op1=ALU.add,
                 )
-            if eng == "V":
-                nc.vector.tensor_copy(out=dst, in_=src)
-            else:
-                nc.gpsimd.tensor_scalar(out=dst, in0=src, scalar1=1.0, scalar2=0.0, op0=ALU.mult, op1=ALU.add)
-
-        def do_QZ2(b, g2, n=None):
-            if n is None:
-                quantise(("z%d" % b, g2, 0), 512, grp[("g", b, g2)][:])
-            elif ROUTE[(b, g2)] == "V":
-                quantise(("z%d" % b, g2, n), 128, grp[("g", b, g2)][:, 512 * n : 512 * n + 512])
-            else:
-                quantise(("z%d" % b, g2, n), 256, grp[("g", b, g2)][:, 1024 * n : 1024 * n + 1024])
-
-        def do_M2(b, n, jh):
-            acc = ps_mm.tile([P, 512], F32, name="acc2", tag="mm")
-            bank[("2", b, n, jh)] = acc
-            for g2 in range(2):
-                if ROUTE[(b, g2)] == "V":
-                    wkey, wcols = ("z%d" % b, g2, n), slice(0, 128)
-                elif RG_HALVES:
-                    wkey, wcols = ("z%d" % b, g2, n // 2), slice(128 * (n % 2), 128 * (n % 2) + 128)
-                else:
-                    wkey, wcols = ("z%d" % b, g2, 0), slice(128 * n, 128 * n + 128)
-                mx(acc[:], wkey, wcols, ("c%d%d" % (b, jh), g2, 0), slice(0, 512), g2 == 0, g2 == 1)
-
-        def do_D(b, n, jh):
-            if (b, n) not in sm:
-                sm[(b, n)] = soft.tile([P, 1024], F32, name="sm", tag="sm")
-            nc.vector.scalar_tensor_tensor(
-                out=sm[(b, n)][:, 512 * jh : 512 * jh + 512].rearrange("p (r c) -> p r c", c=4),
-                in0=cbm[:, 1024 * b + 512 * jh : 1024 * b + 512 * jh + 512].rearrange("p (r c) -> p r c", c=4),
-                scalar=s10k[:, 4 * b + n : 4 * b + n + 1],
-                in1=bank[("2", b, n, jh)][:].rearrange("p (c r) -> p r c", c=4),
-                op0=ALU.mult,
-                op1=ALU.add,
+            negative_max[(b, n)] = stats.tile([P, 1], F32, name="negative_max")
+            nc.vector.tensor_reduce(
+                out=negative_max[(b, n)][:], in_=score[(b, n)][:], axis=AX.X, op=ALU.max, negate=True
             )
 
-        def do_E(b, n):
-            tiny[("m", b, n)] = small.tile([P, 1], F32, name="nmx", tag="nmx")
-            nc.vector.tensor_reduce(out=tiny[("m", b, n)][:], in_=sm[(b, n)][:], axis=AX.X, op=ALU.max, negate=True)
-
-        def do_F(b, n):
-            tiny[("s", b, n)] = small.tile([P, 1], F32, name="ssum", tag="ssum")
-            s = sm[(b, n)]
+        def exponentials(b, n):
+            row_sum[(b, n)] = stats.tile([P, 1], F32, name="row_sum")
             nc.scalar.activation(
-                out=s[:], in_=s[:], func=ACT.Exp, bias=tiny[("m", b, n)][:], scale=1.0, accum_out=tiny[("s", b, n)][:]
+                out=score[(b, n)][:],
+                in_=score[(b, n)][:],
+                func=ACT.Exp,
+                bias=negative_max[(b, n)][:],
+                scale=1.0,
+                accum_out=row_sum[(b, n)][:],
             )
 
-        def do_R(b, n):
-            tiny[("r", b, n)] = small.tile([P, 1], F32, name="rs", tag="rs")
-            nc.vector.reciprocal(tiny[("r", b, n)][:], tiny[("s", b, n)][:])
+        def reciprocal(b, n):
+            inverse_sum[(b, n)] = stats.tile([P, 1], F32, name="inverse_sum")
+            nc.vector.reciprocal(inverse_sum[(b, n)][:], row_sum[(b, n)][:])
 
-        def do_G(b, n, *rest):
-            eng = rest[-1]
-            cols = slice(0, 1024) if len(rest) == 1 else slice(512 * rest[0], 512 * rest[0] + 512)
-            s = sm[(b, n)][:, cols]
-            rs = tiny[("r", b, n)]
-            if eng == "S":
-                nc.scalar.activation(out=s, in_=s, func=ACT.Copy, scale=rs[:])
-            elif eng == "V":
-                nc.vector.tensor_scalar(out=s, in0=s, scalar1=rs[:], scalar2=None, op0=ALU.mult)
+        def normalise_and_store(b, n, on_vector):
+            weights = score[(b, n)]
+            if on_vector:
+                nc.vector.tensor_scalar(
+                    out=weights[:], in0=weights[:], scalar1=inverse_sum[(b, n)][:], scalar2=None, op0=ALU.mult
+                )
             else:
-                nc.gpsimd.tensor_scalar(out=s, in0=s, scalar1=rs[:], scalar2=0.0, op0=ALU.mult, op1=ALU.add)
+                nc.gpsimd.tensor_scalar(
+                    out=weights[:], in0=weights[:], scalar1=inverse_sum[(b, n)][:], scalar2=0.0,
+                    op0=ALU.mult, op1=ALU.add,
+                )
+            nc.sync.dma_start(out=out[b].rearrange("(p n) j -> p n j", n=4)[:, n, :], in_=weights[:])
 
-        def do_ST(b, n, *rest):
-            cols = slice(0, 1024) if len(rest) == 0 else slice(512 * rest[0], 512 * rest[0] + 512)
-            nc.sync.dma_start(out=out[b].rearrange("(p n) j -> p n j", n=4)[:, n, cols], in_=sm[(b, n)][:, cols])
+        for group in GROUPS:
+            for half in range(2):
+                load(group, half)
+                if (group, half) == ("q0", 0):
+                    nc.sync.dma_start(out=bits_row[:], in_=context_bit.rearrange("(o b) j -> o (b j)", o=1))
+                if (group, half) == ("w0", 1):
+                    nc.sync.dma_start(
+                        out=bias_bf16[:].rearrange("p (k v) -> p k v", k=4),
+                        in_=b_in.rearrange("(k p v) -> p k v", k=4, v=2),
+                    )
+                    nc.sync.dma_start(
+                        out=query_bits[:].rearrange("p (b n) -> p b n", b=2),
+                        in_=query_bit.rearrange("b (p n) -> p b n", n=4),
+                    )
 
-        table = {
-            "L": do_L, "LB": do_LB, "BM": do_BM, "BX": do_BX, "TP": do_TP, "EX": do_EX, "QZ": do_QZ, "M1": do_M1,
-            "X1": do_X1, "RG": do_RG, "QZ2": do_QZ2, "M2": do_M2, "D": do_D, "E": do_E, "F": do_F, "R": do_R,
-            "G": do_G, "ST": do_ST, "CB": do_CB, "CS": do_CS, "CM": do_CM,
-        }
-        for step in ORDER:
-            table[step[0]](*step[1:])
+        make_mask_row()
+        prepare("q0", 0, True)
+        prepare("q0", 1, True)
+        spread_mask()
+        quantise_group("q0")
+        copy_mask(0, True)
+        prepare("w0", 0, True)
+        prepare("w0", 1, False)
+        quantise_group("w0")
+        prepare("w1", 0, True)
+        prepare("w1", 1, True)
+        quantise_group("w1")
+        copy_mask(1, False)
+        nc.vector.tensor_copy(out=bias[:], in_=bias_bf16[:])
+
+        project_on_vector(0, 0, 0)
+        project_on_vector(0, 0, 1)
+        prepare("c00", 0, False)
+        prepare("c00", 1, False)
+        project_on_vector(0, 1, 0)
+        quantise_group("c00")
+        prepare("c01", 0, False)
+        prepare("c01", 1, False)
+        project_on_vector(0, 1, 1)
+        quantise_group("c01")
+        prepare("q1", 0, False)
+        prepare("q1", 1, False)
+        prepare("c10", 0, False)
+        quantise_group("q1")
+        nc.vector.tensor_scalar(out=penalty[:], in0=query_bits[:], scalar1=MASKED, scalar2=None, op0=ALU.mult)
+
+        scores(0, 0)
+        prepare("c10", 1, False)
+        scores(0, 1)
+        quantise_group("c10")
+        project_on_scalar(1, 0)
+        exponentials(0, 0)
+        scores(0, 2)
+        quantise_q(1, 0)
+        reciprocal(0, 0)
+        project_on_scalar(1, 1)
+        exponentials(0, 1)
+        scores(0, 3)
+        reciprocal(0, 1)
+        quantise_q(1, 1)
+        prepare("c11", 0, False)
+        prepare("c11", 1, False)
+        quantise_group("c11")
+        exponentials(0, 2)
+        exponentials(0, 3)
+        reciprocal(0, 2)
+        for n in range(3):
+            normalise_and_store(0, n, False)
+
+        before = (0, 3)
+        for n in range(4):
+            scores(1, n)
+            reciprocal(before[0], before[1])
+            normalise_and_store(before[0], before[1], n == 3)
+            exponentials(1, n)
+            before = (1, n)
+        reciprocal(before[0], before[1])
+        normalise_and_store(before[0], before[1], True)

from contextlib import ExitStack

import concourse.mybir as mybir
from concourse.masks import make_identity

F32 = mybir.dt.float32
BF16 = mybir.dt.bfloat16
U32 = mybir.dt.uint32
U8 = mybir.dt.uint8
FP8X4 = mybir.dt.float8_e4m3fn_x4
ALU = mybir.AluOpType
ACT = mybir.ActivationFunctionType
AX = mybir.AxisListType

P = 128
BANK = 512
FEATURES = 1024
CONTEXT_ROWS = 1024
MASKED = 10000.0

GROUPS = ["q0", "w0", "w1", "c00", "c01", "q1", "c10", "c11"]

FLOPS = 2 * 1024 * 1024 * 1024 + 2 * 2 * 512 * 1024 * 1024


def tile_attention_pa_kernel(tc, query, context, query_bit, context_bit, W_in, b_in, out):
    nc = tc.nc
    with ExitStack() as ctx:
        const = ctx.enter_context(tc.tile_pool(name="const", bufs=1))
        loaded = ctx.enter_context(tc.tile_pool(name="loaded", bufs=1))
        packed = ctx.enter_context(tc.tile_pool(name="packed", bufs=1))
        staging = ctx.enter_context(tc.tile_pool(name="staging", bufs=8))
        soft = ctx.enter_context(tc.tile_pool(name="soft", bufs=8))
        stats = ctx.enter_context(tc.tile_pool(name="stats", bufs=8))
        turned = ctx.enter_context(tc.psum_pool(name="turned", bufs=4))
        sums = ctx.enter_context(tc.psum_pool(name="sums", bufs=4))
        ctx.enter_context(tc.manual_schedule())

        warm = const.tile([P, 2], F32, name="warm")
        nc.vector.memset(warm[:], 0.0)
        nc.scalar.activation(out=warm[:, 1:2], in_=warm[:, 0:1], func=ACT.Exp)

        mask_rows = const.tile([P, 2 * CONTEXT_ROWS], BF16, name="mask_rows")
        nc.vector.memset(mask_rows[:], 0.0)
        ones = const.tile([P, P], BF16, name="ones")
        nc.vector.memset(ones[:], 1.0)
        identity = const.tile([P, P], F32, name="identity")
        make_identity(nc, identity[:])
        bits_row = const.tile([1, 2 * CONTEXT_ROWS], BF16, name="bits_row")
        mask = const.tile([P, 2 * CONTEXT_ROWS], BF16, name="mask")
        bias_bf16 = const.tile([P, 8], BF16, name="bias_bf16")
        bias = const.tile([P, 8], F32, name="bias")
        query_bits = const.tile([P, 8], BF16, name="query_bits")
        penalty = const.tile([P, 8], F32, name="penalty")

        raw = {}
        grouped = {}
        codes = {}
        scales = {}
        mask_bank = {}
        q_planes = {}
        q_grouped = {}
        q_words = {}
        score = {}
        negative_max = {}
        row_sum = {}
        inverse_sum = {}

        def load(group, half):
            if half == 0:
                raw[group] = loaded.tile([P, 4 * FEATURES], BF16, name="raw_" + group)
            if group[0] == "q":
                rows = query[int(group[1])].rearrange("(p n) d -> p n d", n=4)[:, 2 * half : 2 * half + 2, :]
            elif group[0] == "w":
                first = 512 * int(group[1]) + 256 * half
                rows = W_in[first : first + 256, :].rearrange("(p v) d -> p v d", v=2)
            else:
                first = 512 * int(group[2])
                rows = context[int(group[1]), first : first + 512, :].rearrange("(p c) e -> p c e", c=4)
                rows = rows[:, 2 * half : 2 * half + 2, :]
            nc.sync.dma_start(
                out=raw[group][:, 2 * FEATURES * half : 2 * FEATURES * (half + 1)].rearrange("p (n k) -> p n k", n=2),
                in_=rows,
            )

        def prepare(group, half, vector_helps):
            words = raw[group][:].bitcast(F32)
            for k_pass in range(2):
                if half == 0:
                    grouped[(group, k_pass)] = staging.tile([P, 4 * BANK], BF16, name="grouped", align_bytes=64)
                bank = turned.tile([P, BANK], F32, name="bank")
                for a in range(2):
                    for u in range(2):
                        first = 512 * (2 * half + a) + 256 * k_pass + 128 * u
                        nc.tensor.transpose(
                            bank[:, (2 * a + u) * P : (2 * a + u + 1) * P], words[:, first : first + P], identity[:]
                        )
                target = grouped[(group, k_pass)][:].bitcast(F32)[:, BANK * half : BANK * (half + 1)]
                target = target.rearrange("p (a r u) -> p a r u", a=2, u=2)
                source = bank[:].rearrange("p (a u r) -> p a r u", a=2, u=2)
                if vector_helps and k_pass == 1:
                    nc.vector.tensor_copy(out=target, in_=source)
                else:
                    nc.scalar.copy(out=target, in_=source)

        def quantise(operand, values):
            width = values.shape[1] // 4
            codes[operand] = packed.tile([P, width], U32, name="codes_%s_%d_%d" % operand, align_bytes=64)
            scales[operand] = packed.tile([P, width], U8, name="scales_%s_%d_%d" % operand, align_bytes=64)
            nc.vector.quantize_mx(out=codes[operand][:].bitcast(FP8X4), scales=scales[operand][:], in_=values)

        def quantise_group(group):
            for k_pass in range(2):
                quantise((group, k_pass, 0), grouped[(group, k_pass)][:])

        def multiply(acc, stationary, stationary_columns, moving, moving_columns, k_pass):
            nc.tensor.matmul_mx(
                out=acc,
                lhsT=codes[stationary][:, stationary_columns].bitcast(FP8X4),
                lhsT_scale=scales[stationary][:, stationary_columns],
                rhs=codes[moving][:, moving_columns].bitcast(FP8X4),
                rhs_scale=scales[moving][:, moving_columns],
                start=(k_pass == 0),
                stop=(k_pass == 1),
            )

        def make_mask_row():
            nc.vector.tensor_scalar(out=mask_rows[0:1, :], in0=bits_row[:], scalar1=-1.0, scalar2=None, op0=ALU.add)

        def spread_mask():
            for b in range(2):
                mask_bank[b] = sums.tile([P, CONTEXT_ROWS], BF16, name="mask_bank", tag="acc")
                for h in range(2):
                    first = CONTEXT_ROWS * b + BANK * h
                    nc.tensor.matmul(
                        out=mask_bank[b][:, BANK * h : BANK * (h + 1)],
                        lhsT=ones[:],
                        rhs=mask_rows[:, first : first + BANK],
                        start=True,
                        stop=True,
                    )

        def copy_mask(b, on_vector):
            target = mask[:, CONTEXT_ROWS * b : CONTEXT_ROWS * (b + 1)]
            if on_vector:
                nc.vector.tensor_copy(out=target, in_=mask_bank[b][:])
            else:
                nc.scalar.copy(out=target, in_=mask_bank[b][:])

        def project_on_vector(b, e_pass, half):
            if half == 0:
                q_grouped[(b, e_pass)] = staging.tile([P, 4 * BANK], BF16, name="q_grouped", bufs=4, align_bytes=64)
            query_tiles = (2 * half, 2 * half + 1)
            acc = {}
            for n in query_tiles:
                acc[n] = sums.tile([P, BANK], F32, name="acc")
                for t in range(4):
                    for d_pass in range(2):
                        multiply(
                            acc[n][:, P * t : P * (t + 1)],
                            ("w%d" % e_pass, d_pass, 0), slice(P * t, P * (t + 1)),
                            ("q%d" % b, d_pass, 0), slice(P * n, P * (n + 1)),
                            d_pass,
                        )
            for n in query_tiles:
                nc.vector.tensor_tensor(
                    out=q_grouped[(b, e_pass)][:, BANK * n : BANK * (n + 1)].rearrange("p (i t) -> p i t", t=4),
                    in0=acc[n][:].rearrange("p (t i) -> p i t", t=4),
                    in1=bias[:, 4 * e_pass : 4 * e_pass + 4].unsqueeze(1).to_broadcast([P, P, 4]),
                    op=ALU.add,
                )
            for n in query_tiles:
                quantise(("z%d" % b, e_pass, n), q_grouped[(b, e_pass)][:, BANK * n : BANK * (n + 1)])
                q_words[(b, e_pass, n)] = (("z%d" % b, e_pass, n), slice(0, P))

        def project_on_scalar(b, e_pass):
            q_planes[(b, e_pass)] = staging.tile([P, 4 * BANK], BF16, name="q_planes", bufs=2)
            q_grouped[(b, e_pass)] = staging.tile([P, 4 * BANK], BF16, name="q_grouped", bufs=4, align_bytes=64)
            for t in range(4):
                acc = sums.tile([P, BANK], F32, name="acc")
                for d_pass in range(2):
                    multiply(
                        acc[:],
                        ("w%d" % e_pass, d_pass, 0), slice(P * t, P * (t + 1)),
                        ("q%d" % b, d_pass, 0), slice(0, BANK),
                        d_pass,
                    )
                nc.scalar.activation(
                    out=q_planes[(b, e_pass)][:, BANK * t : BANK * (t + 1)],
                    in_=acc[:],
                    func=ACT.Identity,
                    bias=bias[:, 4 * e_pass + t : 4 * e_pass + t + 1],
                    scale=1.0,
                )
            planes = q_planes[(b, e_pass)][:].rearrange("p (t i) -> p t i", t=4)
            for half in range(2):
                target = q_grouped[(b, e_pass)][:, 2 * BANK * half : 2 * BANK * (half + 1)]
                nc.gpsimd.tensor_scalar(
                    out=target.rearrange("p (m f t) -> p m t f", f=4, t=4),
                    in0=planes[:, :, 2 * P * half : 2 * P * (half + 1)].rearrange("p t (m f) -> p m t f", f=4),
                    scalar1=1.0,
                    scalar2=0.0,
                    op0=ALU.mult,
                    op1=ALU.add,
                )

        def quantise_q(b, e_pass):
            for half in range(2):
                operand = ("z%d" % b, e_pass, half)
                quantise(operand, q_grouped[(b, e_pass)][:, 2 * BANK * half : 2 * BANK * (half + 1)])
                for a in range(2):
                    q_words[(b, e_pass, 2 * half + a)] = (operand, slice(P * a, P * (a + 1)))

        def scores(b, n):
            score[(b, n)] = soft.tile([P, CONTEXT_ROWS], F32, name="score")
            for h in range(2):
                acc = sums.tile([P, BANK], F32, name="acc")
                for e_pass in range(2):
                    operand, columns = q_words[(b, e_pass, n)]
                    multiply(acc[:], operand, columns, ("c%d%d" % (b, h), e_pass, 0), slice(0, BANK), e_pass)
                first = CONTEXT_ROWS * b + BANK * h
                nc.vector.scalar_tensor_tensor(
                    out=score[(b, n)][:, BANK * h : BANK * (h + 1)].rearrange("p (r c) -> p r c", c=4),
                    in0=mask[:, first : first + BANK].rearrange("p (r c) -> p r c", c=4),
                    scalar=penalty[:, 4 * b + n : 4 * b + n + 1],
                    in1=acc[:].rearrange("p (c r) -> p r c", c=4),
                    op0=ALU.mult,
                    op1=ALU.add,
                )
            negative_max[(b, n)] = stats.tile([P, 1], F32, name="negative_max")
            nc.vector.tensor_reduce(
                out=negative_max[(b, n)][:], in_=score[(b, n)][:], axis=AX.X, op=ALU.max, negate=True
            )

        def exponentials(b, n):
            row_sum[(b, n)] = stats.tile([P, 1], F32, name="row_sum")
            nc.scalar.activation(
                out=score[(b, n)][:],
                in_=score[(b, n)][:],
                func=ACT.Exp,
                bias=negative_max[(b, n)][:],
                scale=1.0,
                accum_out=row_sum[(b, n)][:],
            )

        def reciprocal(b, n):
            inverse_sum[(b, n)] = stats.tile([P, 1], F32, name="inverse_sum")
            nc.vector.reciprocal(inverse_sum[(b, n)][:], row_sum[(b, n)][:])

        def normalise_and_store(b, n, on_vector):
            weights = score[(b, n)]
            if on_vector:
                nc.vector.tensor_scalar(
                    out=weights[:], in0=weights[:], scalar1=inverse_sum[(b, n)][:], scalar2=None, op0=ALU.mult
                )
            else:
                nc.gpsimd.tensor_scalar(
                    out=weights[:], in0=weights[:], scalar1=inverse_sum[(b, n)][:], scalar2=0.0,
                    op0=ALU.mult, op1=ALU.add,
                )
            nc.sync.dma_start(out=out[b].rearrange("(p n) j -> p n j", n=4)[:, n, :], in_=weights[:])

        for group in GROUPS:
            for half in range(2):
                load(group, half)
                if (group, half) == ("q0", 0):
                    nc.sync.dma_start(out=bits_row[:], in_=context_bit.rearrange("(o b) j -> o (b j)", o=1))
                if (group, half) == ("w0", 1):
                    nc.sync.dma_start(
                        out=bias_bf16[:].rearrange("p (k v) -> p k v", k=4),
                        in_=b_in.rearrange("(k p v) -> p k v", k=4, v=2),
                    )
                    nc.sync.dma_start(
                        out=query_bits[:].rearrange("p (b n) -> p b n", b=2),
                        in_=query_bit.rearrange("b (p n) -> p b n", n=4),
                    )

        make_mask_row()
        prepare("q0", 0, True)
        prepare("q0", 1, True)
        spread_mask()
        quantise_group("q0")
        copy_mask(0, True)
        prepare("w0", 0, True)
        prepare("w0", 1, False)
        quantise_group("w0")
        prepare("w1", 0, True)
        prepare("w1", 1, True)
        quantise_group("w1")
        copy_mask(1, False)
        nc.vector.tensor_copy(out=bias[:], in_=bias_bf16[:])

        project_on_vector(0, 0, 0)
        project_on_vector(0, 0, 1)
        prepare("c00", 0, False)
        prepare("c00", 1, False)
        project_on_vector(0, 1, 0)
        quantise_group("c00")
        prepare("c01", 0, False)
        prepare("c01", 1, False)
        project_on_vector(0, 1, 1)
        quantise_group("c01")
        prepare("q1", 0, False)
        prepare("q1", 1, False)
        prepare("c10", 0, False)
        quantise_group("q1")
        nc.vector.tensor_scalar(out=penalty[:], in0=query_bits[:], scalar1=MASKED, scalar2=None, op0=ALU.mult)

        scores(0, 0)
        prepare("c10", 1, False)
        scores(0, 1)
        quantise_group("c10")
        project_on_scalar(1, 0)
        exponentials(0, 0)
        scores(0, 2)
        quantise_q(1, 0)
        reciprocal(0, 0)
        project_on_scalar(1, 1)
        exponentials(0, 1)
        scores(0, 3)
        reciprocal(0, 1)
        quantise_q(1, 1)
        prepare("c11", 0, False)
        prepare("c11", 1, False)
        quantise_group("c11")
        exponentials(0, 2)
        exponentials(0, 3)
        reciprocal(0, 2)
        for n in range(3):
            normalise_and_store(0, n, False)

        before = (0, 3)
        for n in range(4):
            scores(1, n)
            reciprocal(before[0], before[1])
            normalise_and_store(before[0], before[1], n == 3)
            exponentials(1, n)
            before = (1, n)
        reciprocal(before[0], before[1])
        normalise_and_store(before[0], before[1], True)
